import numpy as np
import ml_dtypes


def mxq(x, axis, fmt="e4m3"):
    dtype, down = {"e4m3": (ml_dtypes.float8_e4m3fn, 7), "e5m2": (ml_dtypes.float8_e5m2, 14)}[fmt]
    v = np.moveaxis(np.asarray(x, np.float32).astype(ml_dtypes.bfloat16).astype(np.float64), axis, -1)
    blocks = v.reshape(v.shape[:-1] + (-1, 32))
    amax = np.abs(blocks).max(-1, keepdims=True)
    byte = np.maximum(np.where(amax > 0, np.frexp(amax)[1] - 1 + 127, 0) - down, 1)
    scale = np.exp2(byte - 127.0)
    codes = (blocks / scale).astype(np.float32).astype(dtype).astype(np.float64)
    return np.moveaxis((codes * scale).reshape(v.shape), -1, axis)


WIDE = False


def mx_kscale(k):
    if not WIDE:
        return np.ones(k)
    levels = np.array([10, -10, 5, -5, 0])
    a = np.random.permutation(np.resize(levels, k // 512 * 4)).reshape(k // 512, 4)
    idx = np.arange(k)
    return np.exp2(a[idx // 512, idx % 128 // 32])


BF16 = ml_dtypes.bfloat16


def bf(x):
    return np.asarray(x, np.float32).astype(BF16)


def f64(x):
    return np.asarray(x).astype(np.float64)


B, N_IN, N_UNITS, N_EXC = 4096, 512, 1024, 512


def setup_inputs():
    k = mx_kscale(N_IN)
    return {
        "x_t": bf(np.random.standard_normal((B, N_IN)) * k),
        "y_exc": bf(np.random.random((B, N_EXC))),
        "s_exc": bf(np.random.random((B, N_EXC))),
        "y_inh": bf(np.random.random((B, N_EXC))),
        "s_inh": bf(np.random.random((B, N_EXC))),
        "iw": bf(np.random.standard_normal((N_IN, N_UNITS)) / np.sqrt(N_IN) / k[:, None]),
        "eiw": bf(np.random.standard_normal((N_EXC, N_EXC)) / np.sqrt(N_EXC)),
        "l": bf(np.random.standard_normal(N_UNITS) * 0.5),
    }


def reference(x_t, y_exc, s_exc, y_inh, s_inh, iw, eiw, l):
    x_t, y_exc, s_exc, y_inh, s_inh = f64(x_t), f64(y_exc), f64(s_exc), f64(y_inh), f64(s_inh)
    iw, eiw, l = f64(iw), f64(eiw), f64(l)
    w_exc, w_inh = iw[:, :N_EXC], iw[:, N_EXC:]
    l_exc, l_inh = l[:N_EXC], l[N_EXC:]
    xq = mxq(x_t, 1, "e4m3")
    s_exc_new = np.maximum(
        (xq @ mxq(w_exc, 0, "e4m3")) + y_exc
        - (mxq(y_inh, 1, "e4m3") @ mxq(-eiw, 0, "e4m3"))
        + l_exc * s_exc * (1.0 - y_exc), 0.0)
    s_inh_new = np.maximum(
        (xq @ mxq(w_inh, 0, "e4m3")) + y_inh
        - (mxq(y_exc, 1, "e4m3") @ mxq(eiw.T, 0, "e4m3"))
        + l_inh * s_inh * (1.0 - y_inh), 0.0)
    return s_exc_new, s_inh_new

@@ -1,0 +1,206 @@
+import concourse.mybir as mybir
+from concourse.masks import make_identity
+
+FP8X4 = mybir.dt.float8_e4m3fn_x4
+BF16 = mybir.dt.bfloat16
+F32 = mybir.dt.float32
+U32 = mybir.dt.uint32
+U8 = mybir.dt.uint8
+ALU = mybir.AluOpType
+ACT = mybir.ActivationFunctionType
+
+P = 128
+PACK = 4
+BATCH = 4096
+K = 512
+UNITS = 512
+SLOTS = 4
+GROUP_ROWS = P * SLOTS
+N_GROUPS = BATCH // GROUP_ROWS
+WORDS = K // 2
+
+FLOPS = 4 * 2 * BATCH * K * UNITS
+
+
+def turn_rows(nc, psum, identity, rows, grouped):
+    words = rows.bitcast(F32)
+    grouped_words = grouped.bitcast(F32).rearrange("p (i r u) -> p i r u", i=SLOTS, u=2)
+    for half in range(SLOTS // 2):
+        turned = psum.tile([P, 2, 2, P], F32, tag="turned")
+        for a in range(2):
+            for u in range(2):
+                first = (2 * half + a) * WORDS + u * P
+                nc.tensor.transpose(turned[:, a, u, :], words[:, first : first + P], identity)
+        nc.scalar.copy(
+            out=grouped_words[:, 2 * half : 2 * half + 2, :, :],
+            in_=turned[:].rearrange("p a u r -> p a r u"),
+        )
+
+
+def load_k_first(nc, raw, weight):
+    for u in range(2):
+        nc.sync.dma_start(
+            out=raw[:, 2 * u : 2 * u + 2, :],
+            in_=weight[256 * u : 256 * u + 256, :].rearrange("(p e) n -> p e n", e=2),
+        )
+
+
+def quantise(nc, codes, scales, grouped):
+    nc.vector.quantize_mx(out=codes.bitcast(FP8X4), scales=scales, in_=grouped)
+
+
+def tile_eisnucell_pa_t_kernel(
+    tc, x_t, y_exc, s_exc, y_inh, s_inh, iw, eiw, l, out_0, out_1
+):
+    nc = tc.nc
+
+    def grouped_view(dram):
+        return dram.rearrange("(g p i) c -> g p (i c)", p=P, i=SLOTS)
+
+    x_groups = grouped_view(x_t)
+    y_groups = {"exc": grouped_view(y_exc), "inh": grouped_view(y_inh)}
+    s_groups = {"exc": grouped_view(s_exc), "inh": grouped_view(s_inh)}
+    out_groups = {"exc": grouped_view(out_0), "inh": grouped_view(out_1)}
+    first_unit = {"exc": 0, "inh": UNITS}
+    other = {"exc": "inh", "inh": "exc"}
+
+    with (
+        tc.tile_pool(name="keep", bufs=1) as keep,
+        tc.tile_pool(name="prepare", bufs=1) as prepare,
+        tc.tile_pool(name="loads", bufs=3) as loads,
+        tc.tile_pool(name="operands", bufs=2) as operands,
+        tc.tile_pool(name="terms", bufs=2) as terms,
+        tc.tile_pool(name="results", bufs=4) as results,
+        tc.psum_pool(name="turn", bufs=3) as turn,
+        tc.psum_pool(name="sums", bufs=4) as sums,
+    ):
+        identity = keep.tile([P, P], F32)
+        make_identity(nc, identity[:])
+
+        raw_iw = prepare.tile([P, PACK, 2 * UNITS], BF16)
+        load_k_first(nc, raw_iw, iw)
+        raw_eiw = prepare.tile([P, PACK, UNITS], BF16)
+        load_k_first(nc, raw_eiw, eiw)
+        eiw_rows = prepare.tile([P, SLOTS * K], BF16)
+        nc.sync.dma_start(
+            out=eiw_rows[:].rearrange("p (c k) -> p c k", c=SLOTS),
+            in_=eiw.rearrange("(c p) k -> p c k", p=P),
+        )
+        leak = keep.tile([P, 2 * UNITS], BF16)
+        nc.gpsimd.dma_start(out=leak[:], in_=l.partition_broadcast(P))
+
+        w_codes, w_scales, r_codes, r_scales = {}, {}, {}, {}
+        for pop in ("exc", "inh"):
+            w_codes[pop] = keep.tile([P, UNITS], U32, name="w_codes_" + pop, align_bytes=64)
+            w_scales[pop] = keep.tile([P, UNITS], U8, name="w_scales_" + pop, align_bytes=64)
+            r_codes[pop] = keep.tile([P, UNITS], U32, name="r_codes_" + pop, align_bytes=64)
+            r_scales[pop] = keep.tile([P, UNITS], U8, name="r_scales_" + pop, align_bytes=64)
+
+        for pop in ("exc", "inh"):
+            cols = slice(first_unit[pop], first_unit[pop] + UNITS)
+            grouped_w = prepare.tile(
+                [P, UNITS, PACK], BF16, name="grouped_w_" + pop, align_bytes=64
+            )
+            nc.vector.tensor_copy(
+                out=grouped_w[:], in_=raw_iw[:, :, cols].rearrange("p t n -> p n t")
+            )
+            quantise(
+                nc,
+                w_codes[pop][:],
+                w_scales[pop][:],
+                grouped_w[:].rearrange("p n t -> p (n t)"),
+            )
+
+        grouped_eiw = prepare.tile([P, UNITS, PACK], BF16, align_bytes=64)
+        nc.vector.tensor_copy(out=grouped_eiw[:], in_=raw_eiw[:].rearrange("p t n -> p n t"))
+        quantise(
+            nc,
+            r_codes["exc"][:],
+            r_scales["exc"][:],
+            grouped_eiw[:].rearrange("p n t -> p (n t)"),
+        )
+
+        minus_eiw_rows = prepare.tile([P, SLOTS * K], BF16)
+        nc.vector.tensor_scalar_mul(out=minus_eiw_rows[:], in0=eiw_rows[:], scalar1=-1.0)
+        grouped_eiw_t = prepare.tile([P, UNITS * PACK], BF16, align_bytes=64)
+        turn_rows(nc, turn, identity[:], minus_eiw_rows[:], grouped_eiw_t[:])
+        quantise(nc, r_codes["inh"][:], r_scales["inh"][:], grouped_eiw_t[:])
+
+        for g in range(N_GROUPS):
+            x_rows = loads.tile([P, SLOTS * K], BF16)
+            nc.sync.dma_start(out=x_rows[:], in_=x_groups[g])
+            y_rows, s_rows = {}, {}
+            for pop in ("exc", "inh"):
+                y_rows[pop] = loads.tile([P, SLOTS * UNITS], BF16, name="y_rows_" + pop)
+                nc.sync.dma_start(out=y_rows[pop][:], in_=y_groups[pop][g])
+            for pop in ("exc", "inh"):
+                s_rows[pop] = loads.tile([P, SLOTS * UNITS], BF16, name="s_rows_" + pop)
+                nc.sync.dma_start(out=s_rows[pop][:], in_=s_groups[pop][g])
+
+            a_codes, a_scales = {}, {}
+            for name, rows in (("x", x_rows), ("exc", y_rows["exc"]), ("inh", y_rows["inh"])):
+                grouped = operands.tile(
+                    [P, GROUP_ROWS * PACK], BF16, name="grouped_" + name, align_bytes=64
+                )
+                turn_rows(nc, turn, identity[:], rows[:], grouped[:])
+                a_codes[name] = operands.tile(
+                    [P, GROUP_ROWS], U32, name="a_codes_" + name, align_bytes=64
+                )
+                a_scales[name] = operands.tile(
+                    [P, GROUP_ROWS], U8, name="a_scales_" + name, align_bytes=64
+                )
+                quantise(nc, a_codes[name][:], a_scales[name][:], grouped[:])
+
+            for pop in ("exc", "inh"):
+                cols = slice(first_unit[pop], first_unit[pop] + UNITS)
+                one_minus_y = terms.tile([P, SLOTS * UNITS], F32)
+                nc.scalar.activation(
+                    out=one_minus_y[:], in_=y_rows[pop][:], func=ACT.Identity, bias=1.0, scale=-1.0
+                )
+                state = results.tile([P, SLOTS, UNITS], F32)
+                nc.vector.tensor_tensor(
+                    out=state[:],
+                    in0=s_rows[pop][:].rearrange("p (i n) -> p i n", i=SLOTS),
+                    in1=leak[:, cols].unsqueeze(1).to_broadcast([P, SLOTS, UNITS]),
+                    op=ALU.mult,
+                )
+                flat_state = state[:].rearrange("p i n -> p (i n)")
+                nc.vector.scalar_tensor_tensor(
+                    out=flat_state,
+                    in0=flat_state,
+                    scalar=1.0,
+                    in1=one_minus_y[:],
+                    op0=ALU.subtract,
+                    op1=ALU.mult,
+                )
+                for i in range(SLOTS):
+                    slot = slice(i * P, (i + 1) * P)
+                    acc = sums.tile([P, UNITS], F32)
+                    nc.tensor.matmul_mx(
+                        out=acc[:],
+                        lhsT=a_codes["x"][:, slot].bitcast(FP8X4),
+                        lhsT_scale=a_scales["x"][:, slot],
+                        rhs=w_codes[pop][:].bitcast(FP8X4),
+                        rhs_scale=w_scales[pop][:],
+                        start=True,
+                        stop=False,
+                    )
+                    nc.tensor.matmul_mx(
+                        out=acc[:],
+                        lhsT=a_codes[other[pop]][:, slot].bitcast(FP8X4),
+                        lhsT_scale=a_scales[other[pop]][:, slot],
+                        rhs=r_codes[pop][:].bitcast(FP8X4),
+                        rhs_scale=r_scales[pop][:],
+                        start=False,
+                        stop=True,
+                    )
+                    nc.vector.scalar_tensor_tensor(
+                        out=state[:, i, :],
+                        in0=acc[:],
+                        scalar=1.0,
+                        in1=state[:, i, :],
+                        op0=ALU.add,
+                        op1=ALU.add,
+                    )
+                    nc.scalar.activation(out=state[:, i, :], in_=state[:, i, :], func=ACT.Relu)
+                nc.scalar.dma_start(out=out_groups[pop][g], in_=flat_state)

@@ -14,39 +14,17 @@ PACK = 4
 BATCH = 4096
 K = 512
 UNITS = 512
+CHUNKS = UNITS // P
 SLOTS = 4
 GROUP_ROWS = P * SLOTS
 N_GROUPS = BATCH // GROUP_ROWS
 WORDS = K // 2
+PSUM_BANKS = 8
+POPS = ("exc", "inh")
+OTHER = {"exc": "inh", "inh": "exc"}
+FIRST_CHUNK = {"exc": 0, "inh": CHUNKS}
 
 FLOPS = 4 * 2 * BATCH * K * UNITS
-
-
-def turn_rows(nc, psum, identity, rows, grouped):
-    words = rows.bitcast(F32)
-    grouped_words = grouped.bitcast(F32).rearrange("p (i r u) -> p i r u", i=SLOTS, u=2)
-    for half in range(SLOTS // 2):
-        turned = psum.tile([P, 2, 2, P], F32, tag="turned")
-        for a in range(2):
-            for u in range(2):
-                first = (2 * half + a) * WORDS + u * P
-                nc.tensor.transpose(turned[:, a, u, :], words[:, first : first + P], identity)
-        nc.scalar.copy(
-            out=grouped_words[:, 2 * half : 2 * half + 2, :, :],
-            in_=turned[:].rearrange("p a u r -> p a r u"),
-        )
-
-
-def load_k_first(nc, raw, weight):
-    for u in range(2):
-        nc.sync.dma_start(
-            out=raw[:, 2 * u : 2 * u + 2, :],
-            in_=weight[256 * u : 256 * u + 256, :].rearrange("(p e) n -> p e n", e=2),
-        )
-
-
-def quantise(nc, codes, scales, grouped):
-    nc.vector.quantize_mx(out=codes.bitcast(FP8X4), scales=scales, in_=grouped)
 
 
 def tile_eisnucell_pa_t_kernel(
@@ -57,150 +35,245 @@ def tile_eisnucell_pa_t_kernel(
     def grouped_view(dram):
         return dram.rearrange("(g p i) c -> g p (i c)", p=P, i=SLOTS)
 
-    x_groups = grouped_view(x_t)
-    y_groups = {"exc": grouped_view(y_exc), "inh": grouped_view(y_inh)}
-    s_groups = {"exc": grouped_view(s_exc), "inh": grouped_view(s_inh)}
-    out_groups = {"exc": grouped_view(out_0), "inh": grouped_view(out_1)}
-    first_unit = {"exc": 0, "inh": UNITS}
-    other = {"exc": "inh", "inh": "exc"}
+    inputs = {
+        "x": grouped_view(x_t),
+        "y_exc": grouped_view(y_exc),
+        "y_inh": grouped_view(y_inh),
+        "s_exc": grouped_view(s_exc),
+        "s_inh": grouped_view(s_inh),
+    }
+    outputs = {"exc": grouped_view(out_0), "inh": grouped_view(out_1)}
 
     with (
         tc.tile_pool(name="keep", bufs=1) as keep,
         tc.tile_pool(name="prepare", bufs=1) as prepare,
         tc.tile_pool(name="loads", bufs=3) as loads,
-        tc.tile_pool(name="operands", bufs=2) as operands,
-        tc.tile_pool(name="terms", bufs=2) as terms,
-        tc.tile_pool(name="results", bufs=4) as results,
-        tc.psum_pool(name="turn", bufs=3) as turn,
-        tc.psum_pool(name="sums", bufs=4) as sums,
+        tc.tile_pool(name="packed", bufs=2) as packed,
+        tc.tile_pool(name="factors", bufs=2) as factors,
+        tc.tile_pool(name="results", bufs=2) as results,
+        tc.psum_pool(name="psum", bufs=PSUM_BANKS) as psum,
+        tc.manual_schedule(),
     ):
-        identity = keep.tile([P, P], F32)
-        make_identity(nc, identity[:])
+        identity_f32 = keep.tile([P, P], F32)
+        make_identity(nc, identity_f32[:])
+        identity_bf16 = keep.tile([P, P], BF16)
+        make_identity(nc, identity_bf16[:])
+
+        def load_group(g):
+            tiles = {}
+            for name in ("x", "y_exc", "y_inh", "s_exc", "s_inh"):
+                tiles[name] = loads.tile([P, SLOTS * K], BF16, name="rows_" + name)
+                nc.sync.dma_start(out=tiles[name][:], in_=inputs[name][g])
+            return tiles
+
+        def turn_rows(rows, grouped, half):
+            words = rows.bitcast(F32)
+            grouped_words = grouped.bitcast(F32).rearrange("p (i r u) -> p i r u", i=SLOTS, u=2)
+            turned = psum.tile([P, 2, 2, P], F32, tag="bank")
+            for a in range(2):
+                for u in range(2):
+                    first = (2 * half + a) * WORDS + u * P
+                    nc.tensor.transpose(
+                        turned[:, a, u, :], words[:, first : first + P], identity_f32[:]
+                    )
+            nc.scalar.copy(
+                out=grouped_words[:, 2 * half : 2 * half + 2, :, :],
+                in_=turned[:].rearrange("p a u r -> p a r u"),
+            )
+
+        def new_operand(name):
+            return {
+                "grouped": packed.tile(
+                    [P, GROUP_ROWS * PACK], BF16, name="grouped_" + name, align_bytes=64
+                ),
+                "codes": packed.tile([P, GROUP_ROWS], U32, name="codes_" + name, align_bytes=64),
+                "scales": packed.tile([P, GROUP_ROWS], U8, name="scales_" + name, align_bytes=64),
+            }
+
+        def quantise(one_operand):
+            nc.vector.quantize_mx(
+                out=one_operand["codes"][:].bitcast(FP8X4),
+                scales=one_operand["scales"][:],
+                in_=one_operand["grouped"][:],
+            )
+
+        def turn_states(s_rows, factor_t, pop, pair):
+            turned = psum.tile([P, 2, SLOTS, P], BF16, tag="bank")
+            for a in range(2):
+                for i in range(SLOTS):
+                    first = i * UNITS + (2 * pair + a) * P
+                    nc.tensor.transpose(
+                        turned[:, a, i, :], s_rows[:, first : first + P], identity_bf16[:]
+                    )
+            for a in range(2):
+                chunk = 2 * pair + a
+                column = FIRST_CHUNK[pop] + chunk
+                nc.scalar.activation(
+                    out=factor_t[:, chunk, :],
+                    in_=turned[:, a, :, :].rearrange("p i r -> p (i r)"),
+                    func=ACT.Identity,
+                    bias=1.0,
+                    scale=minus_l[:, column : column + 1],
+                )
+
+        def leak_term(factor_t, y_rows, state, i):
+            factor = psum.tile([P, UNITS], F32, tag="bank")
+            for chunk in range(CHUNKS):
+                nc.tensor.transpose(
+                    factor[:, chunk * P : (chunk + 1) * P],
+                    factor_t[:, chunk, i * P : (i + 1) * P],
+                    identity_f32[:],
+                )
+            nc.vector.scalar_tensor_tensor(
+                out=state[:, i, :],
+                in0=y_rows[:, i * UNITS : (i + 1) * UNITS],
+                scalar=1.0,
+                in1=factor[:],
+                op0=ALU.subtract,
+                op1=ALU.mult,
+            )
+
+        def new_state(group_operand, pop, state, i):
+            slot = slice(i * P, (i + 1) * P)
+            acc = psum.tile([P, UNITS], F32, tag="bank")
+            nc.tensor.matmul_mx(
+                out=acc[:],
+                lhsT=group_operand["x"]["codes"][:, slot].bitcast(FP8X4),
+                lhsT_scale=group_operand["x"]["scales"][:, slot],
+                rhs=w_codes[pop][:].bitcast(FP8X4),
+                rhs_scale=w_scales[pop][:],
+                start=True,
+                stop=False,
+            )
+            nc.tensor.matmul_mx(
+                out=acc[:],
+                lhsT=group_operand[OTHER[pop]]["codes"][:, slot].bitcast(FP8X4),
+                lhsT_scale=group_operand[OTHER[pop]]["scales"][:, slot],
+                rhs=r_codes[pop][:].bitcast(FP8X4),
+                rhs_scale=r_scales[pop][:],
+                start=False,
+                stop=True,
+            )
+            nc.vector.scalar_tensor_tensor(
+                out=state[:, i, :],
+                in0=acc[:],
+                scalar=1.0,
+                in1=state[:, i, :],
+                op0=ALU.add,
+                op1=ALU.add,
+            )
+            nc.scalar.activation(out=state[:, i, :], in_=state[:, i, :], func=ACT.Relu)
+
+        l_rows = prepare.tile([P, P], BF16)
+        nc.vector.memset(l_rows[:], 0.0)
+        nc.sync.dma_start(out=l_rows[0 : 2 * CHUNKS, :], in_=l.rearrange("(c u) -> c u", u=P))
+        loaded = {0: load_group(0)}
 
         raw_iw = prepare.tile([P, PACK, 2 * UNITS], BF16)
-        load_k_first(nc, raw_iw, iw)
         raw_eiw = prepare.tile([P, PACK, UNITS], BF16)
-        load_k_first(nc, raw_eiw, eiw)
+        for raw, weight in ((raw_iw, iw), (raw_eiw, eiw)):
+            for u in range(2):
+                nc.sync.dma_start(
+                    out=raw[:, 2 * u : 2 * u + 2, :],
+                    in_=weight[256 * u : 256 * u + 256, :].rearrange("(p e) n -> p e n", e=2),
+                )
         eiw_rows = prepare.tile([P, SLOTS * K], BF16)
         nc.sync.dma_start(
             out=eiw_rows[:].rearrange("p (c k) -> p c k", c=SLOTS),
             in_=eiw.rearrange("(c p) k -> p c k", p=P),
         )
-        leak = keep.tile([P, 2 * UNITS], BF16)
-        nc.gpsimd.dma_start(out=leak[:], in_=l.partition_broadcast(P))
+        loaded[1] = load_group(1)
+
+        l_turned = psum.tile([P, P], BF16, tag="bank")
+        nc.tensor.transpose(l_turned[:], l_rows[:], identity_bf16[:])
+        minus_l = keep.tile([P, 2 * CHUNKS], F32)
+        nc.scalar.mul(out=minus_l[:], in_=l_turned[:, 0 : 2 * CHUNKS], mul=-1.0)
+
+        operand = {0: {}}
+        factor_t = {0: {}}
+        for name, source in (("x", "x"), ("exc", "y_exc"), ("inh", "y_inh")):
+            operand[0][name] = new_operand(name)
+            for half in range(SLOTS // 2):
+                turn_rows(loaded[0][source][:], operand[0][name]["grouped"][:], half)
+        for name in ("x", "exc", "inh"):
+            quantise(operand[0][name])
+        for pop in POPS:
+            factor_t[0][pop] = factors.tile([P, CHUNKS, GROUP_ROWS], F32, name="factor_t_" + pop)
+            for pair in range(CHUNKS // 2):
+                turn_states(loaded[0]["s_" + pop][:], factor_t[0][pop], pop, pair)
 
         w_codes, w_scales, r_codes, r_scales = {}, {}, {}, {}
-        for pop in ("exc", "inh"):
+        for pop in POPS:
             w_codes[pop] = keep.tile([P, UNITS], U32, name="w_codes_" + pop, align_bytes=64)
             w_scales[pop] = keep.tile([P, UNITS], U8, name="w_scales_" + pop, align_bytes=64)
             r_codes[pop] = keep.tile([P, UNITS], U32, name="r_codes_" + pop, align_bytes=64)
             r_scales[pop] = keep.tile([P, UNITS], U8, name="r_scales_" + pop, align_bytes=64)
 
-        for pop in ("exc", "inh"):
-            cols = slice(first_unit[pop], first_unit[pop] + UNITS)
-            grouped_w = prepare.tile(
-                [P, UNITS, PACK], BF16, name="grouped_w_" + pop, align_bytes=64
-            )
-            nc.vector.tensor_copy(
-                out=grouped_w[:], in_=raw_iw[:, :, cols].rearrange("p t n -> p n t")
-            )
-            quantise(
-                nc,
-                w_codes[pop][:],
-                w_scales[pop][:],
-                grouped_w[:].rearrange("p n t -> p (n t)"),
-            )
-
-        grouped_eiw = prepare.tile([P, UNITS, PACK], BF16, align_bytes=64)
-        nc.vector.tensor_copy(out=grouped_eiw[:], in_=raw_eiw[:].rearrange("p t n -> p n t"))
-        quantise(
-            nc,
-            r_codes["exc"][:],
-            r_scales["exc"][:],
-            grouped_eiw[:].rearrange("p n t -> p (n t)"),
-        )
-
         minus_eiw_rows = prepare.tile([P, SLOTS * K], BF16)
         nc.vector.tensor_scalar_mul(out=minus_eiw_rows[:], in0=eiw_rows[:], scalar1=-1.0)
         grouped_eiw_t = prepare.tile([P, UNITS * PACK], BF16, align_bytes=64)
-        turn_rows(nc, turn, identity[:], minus_eiw_rows[:], grouped_eiw_t[:])
-        quantise(nc, r_codes["inh"][:], r_scales["inh"][:], grouped_eiw_t[:])
+        for half in range(SLOTS // 2):
+            turn_rows(minus_eiw_rows[:], grouped_eiw_t[:], half)
+
+        grouped_w = {}
+        for pop in POPS:
+            first = FIRST_CHUNK[pop] * P
+            grouped_w[pop] = prepare.tile(
+                [P, UNITS, PACK], BF16, name="grouped_w_" + pop, align_bytes=64
+            )
+            nc.vector.tensor_copy(
+                out=grouped_w[pop][:],
+                in_=raw_iw[:, :, first : first + UNITS].rearrange("p t n -> p n t"),
+            )
+        grouped_eiw = prepare.tile([P, UNITS, PACK], BF16, align_bytes=64)
+        nc.vector.tensor_copy(out=grouped_eiw[:], in_=raw_eiw[:].rearrange("p t n -> p n t"))
+
+        for codes, scales, grouped in (
+            (w_codes["exc"], w_scales["exc"], grouped_w["exc"][:].rearrange("p n t -> p (n t)")),
+            (w_codes["inh"], w_scales["inh"], grouped_w["inh"][:].rearrange("p n t -> p (n t)")),
+            (r_codes["exc"], r_scales["exc"], grouped_eiw[:].rearrange("p n t -> p (n t)")),
+            (r_codes["inh"], r_scales["inh"], grouped_eiw_t[:]),
+        ):
+            nc.vector.quantize_mx(out=codes[:].bitcast(FP8X4), scales=scales[:], in_=grouped)
 
         for g in range(N_GROUPS):
-            x_rows = loads.tile([P, SLOTS * K], BF16)
-            nc.sync.dma_start(out=x_rows[:], in_=x_groups[g])
-            y_rows, s_rows = {}, {}
-            for pop in ("exc", "inh"):
-                y_rows[pop] = loads.tile([P, SLOTS * UNITS], BF16, name="y_rows_" + pop)
-                nc.sync.dma_start(out=y_rows[pop][:], in_=y_groups[pop][g])
-            for pop in ("exc", "inh"):
-                s_rows[pop] = loads.tile([P, SLOTS * UNITS], BF16, name="s_rows_" + pop)
-                nc.sync.dma_start(out=s_rows[pop][:], in_=s_groups[pop][g])
+            ahead = g + 1 < N_GROUPS
+            if g + 2 < N_GROUPS:
+                loaded[g + 2] = load_group(g + 2)
 
-            a_codes, a_scales = {}, {}
-            for name, rows in (("x", x_rows), ("exc", y_rows["exc"]), ("inh", y_rows["inh"])):
-                grouped = operands.tile(
-                    [P, GROUP_ROWS * PACK], BF16, name="grouped_" + name, align_bytes=64
-                )
-                turn_rows(nc, turn, identity[:], rows[:], grouped[:])
-                a_codes[name] = operands.tile(
-                    [P, GROUP_ROWS], U32, name="a_codes_" + name, align_bytes=64
-                )
-                a_scales[name] = operands.tile(
-                    [P, GROUP_ROWS], U8, name="a_scales_" + name, align_bytes=64
-                )
-                quantise(nc, a_codes[name][:], a_scales[name][:], grouped[:])
-
-            for pop in ("exc", "inh"):
-                cols = slice(first_unit[pop], first_unit[pop] + UNITS)
-                one_minus_y = terms.tile([P, SLOTS * UNITS], F32)
-                nc.scalar.activation(
-                    out=one_minus_y[:], in_=y_rows[pop][:], func=ACT.Identity, bias=1.0, scale=-1.0
-                )
-                state = results.tile([P, SLOTS, UNITS], F32)
-                nc.vector.tensor_tensor(
-                    out=state[:],
-                    in0=s_rows[pop][:].rearrange("p (i n) -> p i n", i=SLOTS),
-                    in1=leak[:, cols].unsqueeze(1).to_broadcast([P, SLOTS, UNITS]),
-                    op=ALU.mult,
-                )
-                flat_state = state[:].rearrange("p i n -> p (i n)")
-                nc.vector.scalar_tensor_tensor(
-                    out=flat_state,
-                    in0=flat_state,
-                    scalar=1.0,
-                    in1=one_minus_y[:],
-                    op0=ALU.subtract,
-                    op1=ALU.mult,
-                )
+            state = {}
+            if ahead:
+                operand[g + 1] = {}
+                factor_t[g + 1] = {}
+                for name in ("x", "exc", "inh"):
+                    operand[g + 1][name] = new_operand(name)
+                for half in range(SLOTS // 2):
+                    turn_rows(loaded[g + 1]["x"][:], operand[g + 1]["x"]["grouped"][:], half)
+            for pop in POPS:
+                state[pop] = results.tile([P, SLOTS, UNITS], F32, name="state_" + pop)
+                if ahead:
+                    factor_t[g + 1][pop] = factors.tile(
+                        [P, CHUNKS, GROUP_ROWS], F32, name="factor_t_" + pop
+                    )
                 for i in range(SLOTS):
-                    slot = slice(i * P, (i + 1) * P)
-                    acc = sums.tile([P, UNITS], F32)
-                    nc.tensor.matmul_mx(
-                        out=acc[:],
-                        lhsT=a_codes["x"][:, slot].bitcast(FP8X4),
-                        lhsT_scale=a_scales["x"][:, slot],
-                        rhs=w_codes[pop][:].bitcast(FP8X4),
-                        rhs_scale=w_scales[pop][:],
-                        start=True,
-                        stop=False,
-                    )
-                    nc.tensor.matmul_mx(
-                        out=acc[:],
-                        lhsT=a_codes[other[pop]][:, slot].bitcast(FP8X4),
-                        lhsT_scale=a_scales[other[pop]][:, slot],
-                        rhs=r_codes[pop][:].bitcast(FP8X4),
-                        rhs_scale=r_scales[pop][:],
-                        start=False,
-                        stop=True,
-                    )
-                    nc.vector.scalar_tensor_tensor(
-                        out=state[:, i, :],
-                        in0=acc[:],
-                        scalar=1.0,
-                        in1=state[:, i, :],
-                        op0=ALU.add,
-                        op1=ALU.add,
-                    )
-                    nc.scalar.activation(out=state[:, i, :], in_=state[:, i, :], func=ACT.Relu)
-                nc.scalar.dma_start(out=out_groups[pop][g], in_=flat_state)
+                    leak_term(factor_t[g][pop], loaded[g]["y_" + pop], state[pop], i)
+                    if ahead and i < SLOTS // 2:
+                        turn_rows(
+                            loaded[g + 1]["y_" + pop][:], operand[g + 1][pop]["grouped"][:], i
+                        )
+                    if ahead and i >= SLOTS // 2:
+                        turn_states(
+                            loaded[g + 1]["s_" + pop][:], factor_t[g + 1][pop], pop, i - SLOTS // 2
+                        )
+                if ahead and pop == "exc":
+                    quantise(operand[g + 1]["x"])
+                if ahead and pop == "inh":
+                    quantise(operand[g + 1]["exc"])
+                    quantise(operand[g + 1]["inh"])
+
+            for pop in POPS:
+                for i in range(SLOTS):
+                    new_state(operand[g], pop, state[pop], i)
+                nc.scalar.dma_start(
+                    out=outputs[pop][g], in_=state[pop][:].rearrange("p i n -> p (i n)")
+                )

@@ -20,6 +20,7 @@ GROUP_ROWS = P * SLOTS
 N_GROUPS = BATCH // GROUP_ROWS
 WORDS = K // 2
 PSUM_BANKS = 8
+RUN_SLOTS = 2
 POPS = ("exc", "inh")
 OTHER = {"exc": "inh", "inh": "exc"}
 FIRST_CHUNK = {"exc": 0, "inh": CHUNKS}
@@ -217,13 +218,13 @@ def tile_eisnucell_pa_t_kernel(
 
         grouped_w = {}
         for pop in POPS:
-            first = FIRST_CHUNK[pop] * P
+            first_unit = FIRST_CHUNK[pop] * P
             grouped_w[pop] = prepare.tile(
                 [P, UNITS, PACK], BF16, name="grouped_w_" + pop, align_bytes=64
             )
             nc.vector.tensor_copy(
                 out=grouped_w[pop][:],
-                in_=raw_iw[:, :, first : first + UNITS].rearrange("p t n -> p n t"),
+                in_=raw_iw[:, :, first_unit : first_unit + UNITS].rearrange("p t n -> p n t"),
             )
         grouped_eiw = prepare.tile([P, UNITS, PACK], BF16, align_bytes=64)
         nc.vector.tensor_copy(out=grouped_eiw[:], in_=raw_eiw[:].rearrange("p t n -> p n t"))
@@ -255,25 +256,34 @@ def tile_eisnucell_pa_t_kernel(
                     factor_t[g + 1][pop] = factors.tile(
                         [P, CHUNKS, GROUP_ROWS], F32, name="factor_t_" + pop
                     )
-                for i in range(SLOTS):
-                    leak_term(factor_t[g][pop], loaded[g]["y_" + pop], state[pop], i)
-                    if ahead and i < SLOTS // 2:
-                        turn_rows(
-                            loaded[g + 1]["y_" + pop][:], operand[g + 1][pop]["grouped"][:], i
-                        )
-                    if ahead and i >= SLOTS // 2:
-                        turn_states(
-                            loaded[g + 1]["s_" + pop][:], factor_t[g + 1][pop], pop, i - SLOTS // 2
-                        )
-                if ahead and pop == "exc":
-                    quantise(operand[g + 1]["x"])
-                if ahead and pop == "inh":
-                    quantise(operand[g + 1]["exc"])
-                    quantise(operand[g + 1]["inh"])
-
-            for pop in POPS:
-                for i in range(SLOTS):
-                    new_state(operand[g], pop, state[pop], i)
-                nc.scalar.dma_start(
-                    out=outputs[pop][g], in_=state[pop][:].rearrange("p i n -> p (i n)")
-                )
+                for first_slot in range(0, SLOTS, RUN_SLOTS):
+                    run = range(first_slot, first_slot + RUN_SLOTS)
+                    for i in run:
+                        leak_term(factor_t[g][pop], loaded[g]["y_" + pop], state[pop], i)
+                        if ahead and i < SLOTS // 2:
+                            turn_rows(
+                                loaded[g + 1]["y_" + pop][:], operand[g + 1][pop]["grouped"][:], i
+                            )
+                        if ahead and i >= SLOTS // 2:
+                            turn_states(
+                                loaded[g + 1]["s_" + pop][:],
+                                factor_t[g + 1][pop],
+                                pop,
+                                i - SLOTS // 2,
+                            )
+                    if ahead and first_slot + RUN_SLOTS == SLOTS:
+                        if pop == "exc":
+                            quantise(operand[g + 1]["x"])
+                        else:
+                            quantise(operand[g + 1]["exc"])
+                            quantise(operand[g + 1]["inh"])
+                    for i in run:
+                        new_state(operand[g], pop, state[pop], i)
+                    nc.scalar.dma_start(
+                        out=outputs[pop][g][
+                            :, first_slot * UNITS : (first_slot + RUN_SLOTS) * UNITS
+                        ],
+                        in_=state[pop][:, first_slot : first_slot + RUN_SLOTS, :].rearrange(
+                            "p i n -> p (i n)"
+                        ),
+                    )

@@ -20,6 +20,7 @@ GROUP_ROWS = P * SLOTS
 N_GROUPS = BATCH // GROUP_ROWS
 WORDS = K // 2
 PSUM_BANKS = 8
+LARGEST_F32 = 3.4028234663852886e38
 RUN_SLOTS = 2
 POPS = ("exc", "inh")
 OTHER = {"exc": "inh", "inh": "exc"}
@@ -163,7 +164,14 @@ def tile_eisnucell_pa_t_kernel(
                 op0=ALU.add,
                 op1=ALU.add,
             )
-            nc.scalar.activation(out=state[:, i, :], in_=state[:, i, :], func=ACT.Relu)
+            nc.gpsimd.tensor_scalar(
+                out=state[:, i, :],
+                in0=state[:, i, :],
+                scalar1=LARGEST_F32,
+                scalar2=0.0,
+                op0=ALU.min,
+                op1=ALU.max,
+            )
 
         l_rows = prepare.tile([P, P], BF16)
         nc.vector.memset(l_rows[:], 0.0)
@@ -279,7 +287,7 @@ def tile_eisnucell_pa_t_kernel(
                             quantise(operand[g + 1]["inh"])
                     for i in run:
                         new_state(operand[g], pop, state[pop], i)
-                    nc.scalar.dma_start(
+                    nc.sync.dma_start(
                         out=outputs[pop][g][
                             :, first_slot * UNITS : (first_slot + RUN_SLOTS) * UNITS
                         ],

@@ -21,7 +21,7 @@ N_GROUPS = BATCH // GROUP_ROWS
 WORDS = K // 2
 PSUM_BANKS = 8
 LARGEST_F32 = 3.4028234663852886e38
-RUN_SLOTS = 2
+RUN_SLOTS = 4
 POPS = ("exc", "inh")
 OTHER = {"exc": "inh", "inh": "exc"}
 FIRST_CHUNK = {"exc": 0, "inh": CHUNKS}

@@ -54,7 +54,6 @@ def tile_eisnucell_pa_t_kernel(
         tc.tile_pool(name="factors", bufs=2) as factors,
         tc.tile_pool(name="results", bufs=2) as results,
         tc.psum_pool(name="psum", bufs=PSUM_BANKS) as psum,
-        tc.manual_schedule(),
     ):
         identity_f32 = keep.tile([P, P], F32)
         make_identity(nc, identity_f32[:])

@@ -57,8 +57,6 @@ def tile_eisnucell_pa_t_kernel(
     ):
         identity_f32 = keep.tile([P, P], F32)
         make_identity(nc, identity_f32[:])
-        identity_bf16 = keep.tile([P, P], BF16)
-        make_identity(nc, identity_bf16[:])
 
         def load_group(g):
             tiles = {}
@@ -99,19 +97,19 @@ def tile_eisnucell_pa_t_kernel(
             )
 
         def turn_states(s_rows, factor_t, pop, pair):
-            turned = psum.tile([P, 2, SLOTS, P], BF16, tag="bank")
-            for a in range(2):
-                for i in range(SLOTS):
-                    first = i * UNITS + (2 * pair + a) * P
-                    nc.tensor.transpose(
-                        turned[:, a, i, :], s_rows[:, first : first + P], identity_bf16[:]
-                    )
-            for a in range(2):
-                chunk = 2 * pair + a
-                column = FIRST_CHUNK[pop] + chunk
+            words = s_rows.bitcast(F32)
+            turned = psum.tile([P, SLOTS * P], F32, tag="bank")
+            for i in range(SLOTS):
+                first = i * WORDS + pair * P
+                nc.tensor.transpose(
+                    turned[:, i * P : (i + 1) * P], words[:, first : first + P], identity_f32[:]
+                )
+            halves = turned[:].bitcast(BF16).rearrange("p (n e) -> p e n", e=2)
+            for e in range(2):
+                column = FIRST_CHUNK[pop] + 2 * pair + e
                 nc.scalar.activation(
-                    out=factor_t[:, chunk, :],
-                    in_=turned[:, a, :, :].rearrange("p i r -> p (i r)"),
+                    out=factor_t[:, 2 * e + pair, :],
+                    in_=halves[:, e, :],
                     func=ACT.Identity,
                     bias=1.0,
                     scale=minus_l[:, column : column + 1],
@@ -126,10 +124,10 @@ def tile_eisnucell_pa_t_kernel(
                     identity_f32[:],
                 )
             nc.vector.scalar_tensor_tensor(
-                out=state[:, i, :],
-                in0=y_rows[:, i * UNITS : (i + 1) * UNITS],
+                out=state[:, i, :].rearrange("p (w e) -> p w e", e=2),
+                in0=y_rows[:, i * UNITS : (i + 1) * UNITS].rearrange("p (w e) -> p w e", e=2),
                 scalar=1.0,
-                in1=factor[:],
+                in1=factor[:].rearrange("p (e w) -> p w e", e=2),
                 op0=ALU.subtract,
                 op1=ALU.mult,
             )
@@ -172,9 +170,11 @@ def tile_eisnucell_pa_t_kernel(
                 op1=ALU.max,
             )
 
-        l_rows = prepare.tile([P, P], BF16)
+        l_rows = prepare.tile([P, P], F32)
         nc.vector.memset(l_rows[:], 0.0)
-        nc.sync.dma_start(out=l_rows[0 : 2 * CHUNKS, :], in_=l.rearrange("(c u) -> c u", u=P))
+        nc.sync.dma_start(
+            out=l_rows[:].bitcast(BF16)[0:CHUNKS, :], in_=l.rearrange("(c k) -> c k", c=CHUNKS)
+        )
         loaded = {0: load_group(0)}
 
         raw_iw = prepare.tile([P, PACK, 2 * UNITS], BF16)
@@ -192,10 +192,12 @@ def tile_eisnucell_pa_t_kernel(
         )
         loaded[1] = load_group(1)
 
-        l_turned = psum.tile([P, P], BF16, tag="bank")
-        nc.tensor.transpose(l_turned[:], l_rows[:], identity_bf16[:])
+        l_turned = psum.tile([P, P], F32, tag="bank")
+        nc.tensor.transpose(l_turned[:], l_rows[:], identity_f32[:])
         minus_l = keep.tile([P, 2 * CHUNKS], F32)
-        nc.scalar.mul(out=minus_l[:], in_=l_turned[:, 0 : 2 * CHUNKS], mul=-1.0)
+        nc.scalar.mul(
+            out=minus_l[:], in_=l_turned[:].bitcast(BF16)[:, 0 : 2 * CHUNKS], mul=-1.0
+        )
 
         operand = {0: {}}
         factor_t = {0: {}}

@@ -20,13 +20,28 @@ GROUP_ROWS = P * SLOTS
 N_GROUPS = BATCH // GROUP_ROWS
 WORDS = K // 2
 PSUM_BANKS = 8
-LARGEST_F32 = 3.4028234663852886e38
-RUN_SLOTS = 4
 POPS = ("exc", "inh")
 OTHER = {"exc": "inh", "inh": "exc"}
+SIGN = {"exc": 1.0, "inh": -1.0}
 FIRST_CHUNK = {"exc": 0, "inh": CHUNKS}
 
 FLOPS = 4 * 2 * BATCH * K * UNITS
+
+
+def row_slots(g, pop):
+    return range(SLOTS - row_slot_count(g, pop), SLOTS)
+
+
+def turned_slots(g, pop):
+    return range(SLOTS - row_slot_count(g, pop))
+
+
+def row_slot_count(g, pop):
+    if g == 0:
+        return 0
+    if g == N_GROUPS - 1:
+        return 1 if pop == "exc" else 0
+    return 1 if pop == "exc" else 0
 
 
 def tile_eisnucell_pa_t_kernel(
@@ -53,19 +68,24 @@ def tile_eisnucell_pa_t_kernel(
         tc.tile_pool(name="packed", bufs=2) as packed,
         tc.tile_pool(name="factors", bufs=2) as factors,
         tc.tile_pool(name="results", bufs=2) as results,
+        tc.tile_pool(name="terms", bufs=2) as terms,
         tc.psum_pool(name="psum", bufs=PSUM_BANKS) as psum,
+        tc.manual_schedule(),
     ):
         identity_f32 = keep.tile([P, P], F32)
         make_identity(nc, identity_f32[:])
 
+        def load_rows(tiles, g, name):
+            tiles[name] = loads.tile([P, SLOTS * K], BF16, name="rows_" + name)
+            nc.sync.dma_start(out=tiles[name][:], in_=inputs[name][g])
+
         def load_group(g):
             tiles = {}
-            for name in ("x", "y_exc", "y_inh", "s_exc", "s_inh"):
-                tiles[name] = loads.tile([P, SLOTS * K], BF16, name="rows_" + name)
-                nc.sync.dma_start(out=tiles[name][:], in_=inputs[name][g])
+            for name in ("x", "y_exc", "s_exc", "y_inh", "s_inh"):
+                load_rows(tiles, g, name)
             return tiles
 
-        def turn_rows(rows, grouped, half):
+        def turn_rows(rows, grouped, half, copy=nc.scalar.copy):
             words = rows.bitcast(F32)
             grouped_words = grouped.bitcast(F32).rearrange("p (i r u) -> p i r u", i=SLOTS, u=2)
             turned = psum.tile([P, 2, 2, P], F32, tag="bank")
@@ -75,7 +95,7 @@ def tile_eisnucell_pa_t_kernel(
                     nc.tensor.transpose(
                         turned[:, a, u, :], words[:, first : first + P], identity_f32[:]
                     )
-            nc.scalar.copy(
+            copy(
                 out=grouped_words[:, 2 * half : 2 * half + 2, :, :],
                 in_=turned[:].rearrange("p a u r -> p a r u"),
             )
@@ -96,10 +116,10 @@ def tile_eisnucell_pa_t_kernel(
                 in_=one_operand["grouped"][:],
             )
 
-        def turn_states(s_rows, factor_t, pop, pair):
+        def turn_states(s_rows, factor_t, pop, pair, slots):
             words = s_rows.bitcast(F32)
-            turned = psum.tile([P, SLOTS * P], F32, tag="bank")
-            for i in range(SLOTS):
+            turned = psum.tile([P, len(slots) * P], F32, tag="bank")
+            for i in slots:
                 first = i * WORDS + pair * P
                 nc.tensor.transpose(
                     turned[:, i * P : (i + 1) * P], words[:, first : first + P], identity_f32[:]
@@ -132,7 +152,45 @@ def tile_eisnucell_pa_t_kernel(
                 op1=ALU.mult,
             )
 
-        def new_state(group_operand, pop, state, i):
+        def new_factor_t(g, pop):
+            columns = len(turned_slots(g, pop)) * P
+            return factors.tile([P, CHUNKS, columns], F32, name="factor_t_" + pop)
+
+        def row_product(rows, g, pop):
+            first_unit = FIRST_CHUNK[pop] * P
+            product = {}
+            for i in row_slots(g, pop):
+                product[i] = terms.tile([P, UNITS], F32, name="row_factor_%s" % pop)
+                nc.gpsimd.tensor_tensor(
+                    out=product[i][:],
+                    in0=rows["s_" + pop][:, i * UNITS : (i + 1) * UNITS],
+                    in1=l_everywhere[:, first_unit : first_unit + UNITS],
+                    op=ALU.mult,
+                )
+            return product
+
+        def row_factors(rows, g, pop, product):
+            term = {}
+            for i in row_slots(g, pop):
+                nc.scalar.activation(
+                    out=product[i][:], in_=product[i][:], func=ACT.Identity, bias=1.0, scale=-1.0
+                )
+                term[i] = terms.tile([P, UNITS], F32, name="row_term_%s" % pop)
+                nc.scalar.activation(
+                    out=term[i][:],
+                    in_=rows["y_" + pop][:, i * UNITS : (i + 1) * UNITS],
+                    func=ACT.Identity,
+                    bias=-1.0,
+                )
+            return term
+
+        def row_leak(g, pop, term, product):
+            for i in row_slots(g, pop):
+                nc.gpsimd.tensor_tensor(
+                    out=term[i][:], in0=term[i][:], in1=product[i][:], op=ALU.mult
+                )
+
+        def new_state(group_operand, pop, state, i, term):
             slot = slice(i * P, (i + 1) * P)
             acc = psum.tile([P, UNITS], F32, tag="bank")
             nc.tensor.matmul_mx(
@@ -156,40 +214,67 @@ def tile_eisnucell_pa_t_kernel(
             nc.vector.scalar_tensor_tensor(
                 out=state[:, i, :],
                 in0=acc[:],
-                scalar=1.0,
-                in1=state[:, i, :],
+                scalar=SIGN[pop],
+                in1=term,
                 op0=ALU.add,
-                op1=ALU.add,
+                op1=ALU.add if pop == "exc" else ALU.subtract,
             )
-            nc.gpsimd.tensor_scalar(
-                out=state[:, i, :],
-                in0=state[:, i, :],
-                scalar1=LARGEST_F32,
-                scalar2=0.0,
-                op0=ALU.min,
-                op1=ALU.max,
+
+        def relu(pop, state, i, on_scalar):
+            if on_scalar:
+                nc.scalar.activation(
+                    out=state[:, i, :], in_=state[:, i, :], func=ACT.Relu, scale=SIGN[pop]
+                )
+            else:
+                nc.gpsimd.tensor_scalar(
+                    out=state[:, i, :],
+                    in0=state[:, i, :],
+                    scalar1=SIGN[pop],
+                    scalar2=0.0,
+                    op0=ALU.mult,
+                    op1=ALU.max,
+                )
+
+        def new_result(pop):
+            return results.tile([P, SLOTS, UNITS], F32, name="state_" + pop)
+
+        def store(g, pop, state, first, end):
+            nc.sync.dma_start(
+                out=outputs[pop][g][:, first * UNITS : end * UNITS],
+                in_=state[:, first:end, :].rearrange("p i n -> p (i n)"),
             )
 
         l_rows = prepare.tile([P, P], F32)
         nc.vector.memset(l_rows[:], 0.0)
-        nc.sync.dma_start(
-            out=l_rows[:].bitcast(BF16)[0:CHUNKS, :], in_=l.rearrange("(c k) -> c k", c=CHUNKS)
-        )
-        loaded = {0: load_group(0)}
-
+        l_row = prepare.tile([P, 2 * UNITS], BF16)
+        nc.gpsimd.memset(l_row[:], 0.0)
         raw_iw = prepare.tile([P, PACK, 2 * UNITS], BF16)
         raw_eiw = prepare.tile([P, PACK, UNITS], BF16)
-        for raw, weight in ((raw_iw, iw), (raw_eiw, eiw)):
+        eiw_rows = prepare.tile([P, SLOTS * K], BF16)
+        loaded = {0: {}}
+
+        def load_k_first(raw, weight):
             for u in range(2):
                 nc.sync.dma_start(
                     out=raw[:, 2 * u : 2 * u + 2, :],
                     in_=weight[256 * u : 256 * u + 256, :].rearrange("(p e) n -> p e n", e=2),
                 )
-        eiw_rows = prepare.tile([P, SLOTS * K], BF16)
+
+        nc.sync.dma_start(
+            out=l_rows[:].bitcast(BF16)[0:CHUNKS, :], in_=l.rearrange("(c k) -> c k", c=CHUNKS)
+        )
+        load_k_first(raw_iw, iw)
+        load_rows(loaded[0], 0, "s_exc")
+        load_rows(loaded[0], 0, "y_exc")
+        load_rows(loaded[0], 0, "x")
+        load_k_first(raw_eiw, eiw)
+        load_rows(loaded[0], 0, "y_inh")
         nc.sync.dma_start(
             out=eiw_rows[:].rearrange("p (c k) -> p c k", c=SLOTS),
             in_=eiw.rearrange("(c p) k -> p c k", p=P),
         )
+        load_rows(loaded[0], 0, "s_inh")
+        nc.sync.dma_start(out=l_row[0:1, :], in_=l.rearrange("(a n) -> a n", a=1))
         loaded[1] = load_group(1)
 
         l_turned = psum.tile([P, P], F32, tag="bank")
@@ -199,19 +284,6 @@ def tile_eisnucell_pa_t_kernel(
             out=minus_l[:], in_=l_turned[:].bitcast(BF16)[:, 0 : 2 * CHUNKS], mul=-1.0
         )
 
-        operand = {0: {}}
-        factor_t = {0: {}}
-        for name, source in (("x", "x"), ("exc", "y_exc"), ("inh", "y_inh")):
-            operand[0][name] = new_operand(name)
-            for half in range(SLOTS // 2):
-                turn_rows(loaded[0][source][:], operand[0][name]["grouped"][:], half)
-        for name in ("x", "exc", "inh"):
-            quantise(operand[0][name])
-        for pop in POPS:
-            factor_t[0][pop] = factors.tile([P, CHUNKS, GROUP_ROWS], F32, name="factor_t_" + pop)
-            for pair in range(CHUNKS // 2):
-                turn_states(loaded[0]["s_" + pop][:], factor_t[0][pop], pop, pair)
-
         w_codes, w_scales, r_codes, r_scales = {}, {}, {}, {}
         for pop in POPS:
             w_codes[pop] = keep.tile([P, UNITS], U32, name="w_codes_" + pop, align_bytes=64)
@@ -219,11 +291,23 @@ def tile_eisnucell_pa_t_kernel(
             r_codes[pop] = keep.tile([P, UNITS], U32, name="r_codes_" + pop, align_bytes=64)
             r_scales[pop] = keep.tile([P, UNITS], U8, name="r_scales_" + pop, align_bytes=64)
 
-        minus_eiw_rows = prepare.tile([P, SLOTS * K], BF16)
-        nc.vector.tensor_scalar_mul(out=minus_eiw_rows[:], in0=eiw_rows[:], scalar1=-1.0)
-        grouped_eiw_t = prepare.tile([P, UNITS * PACK], BF16, align_bytes=64)
-        for half in range(SLOTS // 2):
-            turn_rows(minus_eiw_rows[:], grouped_eiw_t[:], half)
+        def quantise_weight(codes, scales, grouped):
+            nc.vector.quantize_mx(out=codes[:].bitcast(FP8X4), scales=scales[:], in_=grouped)
+
+        def first_operand(name, source, copy=nc.scalar.copy):
+            operand[0][name] = new_operand(name)
+            for half in range(SLOTS // 2):
+                turn_rows(loaded[0][source][:], operand[0][name]["grouped"][:], half, copy)
+
+        def first_states(pop):
+            factor_t[0][pop] = new_factor_t(0, pop)
+            for pair in range(CHUNKS // 2):
+                turn_states(
+                    loaded[0]["s_" + pop][:], factor_t[0][pop], pop, pair, turned_slots(0, pop)
+                )
+
+        operand = {0: {}}
+        factor_t = {0: {}}
 
         grouped_w = {}
         for pop in POPS:
@@ -231,68 +315,101 @@ def tile_eisnucell_pa_t_kernel(
             grouped_w[pop] = prepare.tile(
                 [P, UNITS, PACK], BF16, name="grouped_w_" + pop, align_bytes=64
             )
-            nc.vector.tensor_copy(
+            nc.vector.tensor_scalar_mul(
                 out=grouped_w[pop][:],
-                in_=raw_iw[:, :, first_unit : first_unit + UNITS].rearrange("p t n -> p n t"),
+                in0=raw_iw[:, :, first_unit : first_unit + UNITS].rearrange("p t n -> p n t"),
+                scalar1=SIGN[pop],
             )
+        first_states("exc")
+        first_operand("exc", "y_exc")
+        for pop in POPS:
+            quantise_weight(
+                w_codes[pop], w_scales[pop], grouped_w[pop][:].rearrange("p n t -> p (n t)")
+            )
+        first_operand("x", "x", nc.vector.tensor_copy)
+        state = {"exc": new_result("exc")}
+        for i in turned_slots(0, "exc"):
+            leak_term(factor_t[0]["exc"], loaded[0]["y_exc"], state["exc"], i)
+        quantise(operand[0]["x"])
         grouped_eiw = prepare.tile([P, UNITS, PACK], BF16, align_bytes=64)
         nc.vector.tensor_copy(out=grouped_eiw[:], in_=raw_eiw[:].rearrange("p t n -> p n t"))
+        quantise(operand[0]["exc"])
+        quantise_weight(
+            r_codes["exc"], r_scales["exc"], grouped_eiw[:].rearrange("p n t -> p (n t)")
+        )
+        first_operand("inh", "y_inh")
+        grouped_eiw_t = prepare.tile([P, UNITS * PACK], BF16, align_bytes=64)
+        for half in range(SLOTS // 2):
+            turn_rows(eiw_rows[:], grouped_eiw_t[:], half)
+        first_states("inh")
+        quantise(operand[0]["inh"])
+        quantise_weight(r_codes["inh"], r_scales["inh"], grouped_eiw_t[:])
+        ones = prepare.tile([P, P], BF16)
+        nc.gpsimd.memset(ones[:], 1.0)
+        l_everywhere = keep.tile([P, 2 * UNITS], BF16)
+        for half in range(2):
+            columns = slice(half * UNITS, (half + 1) * UNITS)
+            spread = psum.tile([P, UNITS], F32, tag="bank")
+            nc.tensor.matmul(spread[:], ones[:], l_row[:, columns], start=True, stop=True)
+            nc.scalar.copy(out=l_everywhere[:, columns], in_=spread[:])
 
-        for codes, scales, grouped in (
-            (w_codes["exc"], w_scales["exc"], grouped_w["exc"][:].rearrange("p n t -> p (n t)")),
-            (w_codes["inh"], w_scales["inh"], grouped_w["inh"][:].rearrange("p n t -> p (n t)")),
-            (r_codes["exc"], r_scales["exc"], grouped_eiw[:].rearrange("p n t -> p (n t)")),
-            (r_codes["inh"], r_scales["inh"], grouped_eiw_t[:]),
-        ):
-            nc.vector.quantize_mx(out=codes[:].bitcast(FP8X4), scales=scales[:], in_=grouped)
+        product, row_term = {}, {}
 
         for g in range(N_GROUPS):
-            ahead = g + 1 < N_GROUPS
+            n = g + 1
+            ahead = n < N_GROUPS
             if g + 2 < N_GROUPS:
                 loaded[g + 2] = load_group(g + 2)
-
-            state = {}
             if ahead:
-                operand[g + 1] = {}
-                factor_t[g + 1] = {}
+                product[n, "exc"] = row_product(loaded[n], n, "exc")
+                operand[n] = {}
+                factor_t[n] = {}
                 for name in ("x", "exc", "inh"):
-                    operand[g + 1][name] = new_operand(name)
+                    operand[n][name] = new_operand(name)
                 for half in range(SLOTS // 2):
-                    turn_rows(loaded[g + 1]["x"][:], operand[g + 1]["x"]["grouped"][:], half)
+                    turn_rows(loaded[n]["x"][:], operand[n]["x"]["grouped"][:], half)
             for pop in POPS:
-                state[pop] = results.tile([P, SLOTS, UNITS], F32, name="state_" + pop)
+                begun = g == 0 and pop == "exc"
+                if not begun:
+                    state[pop] = new_result(pop)
                 if ahead:
-                    factor_t[g + 1][pop] = factors.tile(
-                        [P, CHUNKS, GROUP_ROWS], F32, name="factor_t_" + pop
-                    )
-                for first_slot in range(0, SLOTS, RUN_SLOTS):
-                    run = range(first_slot, first_slot + RUN_SLOTS)
-                    for i in run:
+                    factor_t[n][pop] = new_factor_t(n, pop)
+                    if pop == "inh":
+                        quantise(operand[n]["exc"])
+                for i in range(SLOTS):
+                    if i in turned_slots(g, pop) and not begun:
                         leak_term(factor_t[g][pop], loaded[g]["y_" + pop], state[pop], i)
-                        if ahead and i < SLOTS // 2:
-                            turn_rows(
-                                loaded[g + 1]["y_" + pop][:], operand[g + 1][pop]["grouped"][:], i
+                    if ahead and i < SLOTS // 2:
+                        turn_rows(
+                            loaded[n]["y_" + pop][:], operand[n][pop]["grouped"][:], i
+                        )
+                    if ahead and i >= SLOTS // 2:
+                        turn_states(
+                            loaded[n]["s_" + pop][:],
+                            factor_t[n][pop],
+                            pop,
+                            i - SLOTS // 2,
+                            turned_slots(n, pop),
+                        )
+                if ahead:
+                    quantise(operand[n]["x" if pop == "exc" else "inh"])
+                    if pop == "inh":
+                        for each in POPS:
+                            row_term[n, each] = row_factors(
+                                loaded[n], n, each, product[n, each]
                             )
-                        if ahead and i >= SLOTS // 2:
-                            turn_states(
-                                loaded[g + 1]["s_" + pop][:],
-                                factor_t[g + 1][pop],
-                                pop,
-                                i - SLOTS // 2,
-                            )
-                    if ahead and first_slot + RUN_SLOTS == SLOTS:
-                        if pop == "exc":
-                            quantise(operand[g + 1]["x"])
-                        else:
-                            quantise(operand[g + 1]["exc"])
-                            quantise(operand[g + 1]["inh"])
-                    for i in run:
-                        new_state(operand[g], pop, state[pop], i)
-                    nc.sync.dma_start(
-                        out=outputs[pop][g][
-                            :, first_slot * UNITS : (first_slot + RUN_SLOTS) * UNITS
-                        ],
-                        in_=state[pop][:, first_slot : first_slot + RUN_SLOTS, :].rearrange(
-                            "p i n -> p (i n)"
-                        ),
-                    )
+                        for each in POPS:
+                            row_leak(n, each, row_term[n, each], product[n, each])
+                for i in range(SLOTS):
+                    if i in turned_slots(g, pop):
+                        term = state[pop][:, i, :]
+                    else:
+                        term = row_term[g, pop][i][:]
+                    new_state(operand[g], pop, state[pop], i, term)
+                    relu(pop, state[pop], i, not ahead or (pop, i) in [])
+                    if not ahead:
+                        store(g, pop, state[pop], i, i + 1)
+                if ahead:
+                    store(g, pop, state[pop], 0, SLOTS)
+                    if pop == "exc":
+                        product[n, "inh"] = row_product(loaded[n], n, "inh")

@@ -20,6 +20,7 @@ GROUP_ROWS = P * SLOTS
 N_GROUPS = BATCH // GROUP_ROWS
 WORDS = K // 2
 PSUM_BANKS = 8
+LARGEST_F32 = 3.4028234663852886e38
 POPS = ("exc", "inh")
 OTHER = {"exc": "inh", "inh": "exc"}
 SIGN = {"exc": 1.0, "inh": -1.0}
@@ -81,7 +82,7 @@ def tile_eisnucell_pa_t_kernel(
 
         def load_group(g):
             tiles = {}
-            for name in ("x", "y_exc", "s_exc", "y_inh", "s_inh"):
+            for name in ("x", "y_inh", "s_exc", "y_exc", "s_inh"):
                 load_rows(tiles, g, name)
             return tiles
 
@@ -213,25 +214,23 @@ def tile_eisnucell_pa_t_kernel(
             )
             nc.vector.scalar_tensor_tensor(
                 out=state[:, i, :],
-                in0=acc[:],
-                scalar=SIGN[pop],
-                in1=term,
+                in0=term,
+                scalar=1.0,
+                in1=acc[:],
                 op0=ALU.add,
                 op1=ALU.add if pop == "exc" else ALU.subtract,
             )
 
-        def relu(pop, state, i, on_scalar):
+        def relu(state, i, on_scalar):
             if on_scalar:
-                nc.scalar.activation(
-                    out=state[:, i, :], in_=state[:, i, :], func=ACT.Relu, scale=SIGN[pop]
-                )
+                nc.scalar.activation(out=state[:, i, :], in_=state[:, i, :], func=ACT.Relu)
             else:
                 nc.gpsimd.tensor_scalar(
                     out=state[:, i, :],
                     in0=state[:, i, :],
-                    scalar1=SIGN[pop],
+                    scalar1=LARGEST_F32,
                     scalar2=0.0,
-                    op0=ALU.mult,
+                    op0=ALU.min,
                     op1=ALU.max,
                 )
 
@@ -366,22 +365,41 @@ def tile_eisnucell_pa_t_kernel(
                 factor_t[n] = {}
                 for name in ("x", "exc", "inh"):
                     operand[n][name] = new_operand(name)
-                for half in range(SLOTS // 2):
-                    turn_rows(loaded[n]["x"][:], operand[n]["x"]["grouped"][:], half)
             for pop in POPS:
-                begun = g == 0 and pop == "exc"
-                if not begun:
-                    state[pop] = new_result(pop)
+                for i in range(SLOTS):
+                    if i in turned_slots(g, pop):
+                        term = state[pop][:, i, :]
+                    else:
+                        term = row_term[g, pop][i][:]
+                    new_state(operand[g], pop, state[pop], i, term)
+                    relu(state[pop], i, not ahead)
+                    if not ahead:
+                        store(g, pop, state[pop], i, i + 1)
+                if ahead:
+                    store(g, pop, state[pop], 0, SLOTS)
+                following = (g, "inh") if pop == "exc" else (n, "exc")
+                if pop == "inh" and not ahead:
+                    break
+                state[following[1]] = new_result(following[1])
                 if ahead:
                     factor_t[n][pop] = new_factor_t(n, pop)
                     if pop == "inh":
-                        quantise(operand[n]["exc"])
+                        quantise(operand[n]["inh"])
                 for i in range(SLOTS):
-                    if i in turned_slots(g, pop) and not begun:
-                        leak_term(factor_t[g][pop], loaded[g]["y_" + pop], state[pop], i)
+                    if i in turned_slots(*following):
+                        leak_term(
+                            factor_t[following[0]][following[1]],
+                            loaded[following[0]]["y_" + following[1]],
+                            state[following[1]],
+                            i,
+                        )
+                    if ahead and pop == "exc" and i < SLOTS // 2:
+                        turn_rows(loaded[n]["x"][:], operand[n]["x"]["grouped"][:], i)
                     if ahead and i < SLOTS // 2:
                         turn_rows(
-                            loaded[n]["y_" + pop][:], operand[n][pop]["grouped"][:], i
+                            loaded[n]["y_" + OTHER[pop]][:],
+                            operand[n][OTHER[pop]]["grouped"][:],
+                            i,
                         )
                     if ahead and i >= SLOTS // 2:
                         turn_states(
@@ -392,24 +410,9 @@ def tile_eisnucell_pa_t_kernel(
                             turned_slots(n, pop),
                         )
                 if ahead:
-                    quantise(operand[n]["x" if pop == "exc" else "inh"])
-                    if pop == "inh":
-                        for each in POPS:
-                            row_term[n, each] = row_factors(
-                                loaded[n], n, each, product[n, each]
-                            )
-                        for each in POPS:
-                            row_leak(n, each, row_term[n, each], product[n, each])
-                for i in range(SLOTS):
-                    if i in turned_slots(g, pop):
-                        term = state[pop][:, i, :]
-                    else:
-                        term = row_term[g, pop][i][:]
-                    new_state(operand[g], pop, state[pop], i, term)
-                    relu(pop, state[pop], i, not ahead or (pop, i) in [])
-                    if not ahead:
-                        store(g, pop, state[pop], i, i + 1)
-                if ahead:
-                    store(g, pop, state[pop], 0, SLOTS)
+                    quantise(operand[n]["x" if pop == "exc" else "exc"])
                     if pop == "exc":
-                        product[n, "inh"] = row_product(loaded[n], n, "inh")
+                        row_term[n, "exc"] = row_factors(
+                            loaded[n], n, "exc", product[n, "exc"]
+                        )
+                        row_leak(n, "exc", row_term[n, "exc"], product[n, "exc"])

@@ -38,11 +38,7 @@ def turned_slots(g, pop):
 
 
 def row_slot_count(g, pop):
-    if g == 0:
-        return 0
-    if g == N_GROUPS - 1:
-        return 1 if pop == "exc" else 0
-    return 1 if pop == "exc" else 0
+    return 0 if g == 0 or pop == "inh" else 1
 
 
 def tile_eisnucell_pa_t_kernel(
@@ -259,20 +255,20 @@ def tile_eisnucell_pa_t_kernel(
                     in_=weight[256 * u : 256 * u + 256, :].rearrange("(p e) n -> p e n", e=2),
                 )
 
+        load_k_first(raw_iw, iw)
         nc.sync.dma_start(
             out=l_rows[:].bitcast(BF16)[0:CHUNKS, :], in_=l.rearrange("(c k) -> c k", c=CHUNKS)
         )
-        load_k_first(raw_iw, iw)
         load_rows(loaded[0], 0, "s_exc")
-        load_rows(loaded[0], 0, "y_exc")
         load_rows(loaded[0], 0, "x")
+        load_rows(loaded[0], 0, "y_exc")
         load_k_first(raw_eiw, eiw)
         load_rows(loaded[0], 0, "y_inh")
+        load_rows(loaded[0], 0, "s_inh")
         nc.sync.dma_start(
             out=eiw_rows[:].rearrange("p (c k) -> p c k", c=SLOTS),
             in_=eiw.rearrange("(c p) k -> p c k", p=P),
         )
-        load_rows(loaded[0], 0, "s_inh")
         nc.sync.dma_start(out=l_row[0:1, :], in_=l.rearrange("(a n) -> a n", a=1))
         loaded[1] = load_group(1)
 
@@ -319,29 +315,31 @@ def tile_eisnucell_pa_t_kernel(
                 in0=raw_iw[:, :, first_unit : first_unit + UNITS].rearrange("p t n -> p n t"),
                 scalar1=SIGN[pop],
             )
+        quantise_weight(
+            w_codes["exc"], w_scales["exc"], grouped_w["exc"][:].rearrange("p n t -> p (n t)")
+        )
         first_states("exc")
-        first_operand("exc", "y_exc")
-        for pop in POPS:
-            quantise_weight(
-                w_codes[pop], w_scales[pop], grouped_w[pop][:].rearrange("p n t -> p (n t)")
-            )
         first_operand("x", "x", nc.vector.tensor_copy)
+        first_operand("exc", "y_exc")
+        quantise_weight(
+            w_codes["inh"], w_scales["inh"], grouped_w["inh"][:].rearrange("p n t -> p (n t)")
+        )
+        quantise(operand[0]["x"])
         state = {"exc": new_result("exc")}
         for i in turned_slots(0, "exc"):
             leak_term(factor_t[0]["exc"], loaded[0]["y_exc"], state["exc"], i)
-        quantise(operand[0]["x"])
         grouped_eiw = prepare.tile([P, UNITS, PACK], BF16, align_bytes=64)
         nc.vector.tensor_copy(out=grouped_eiw[:], in_=raw_eiw[:].rearrange("p t n -> p n t"))
-        quantise(operand[0]["exc"])
         quantise_weight(
             r_codes["exc"], r_scales["exc"], grouped_eiw[:].rearrange("p n t -> p (n t)")
         )
         first_operand("inh", "y_inh")
+        quantise(operand[0]["inh"])
+        first_states("inh")
         grouped_eiw_t = prepare.tile([P, UNITS * PACK], BF16, align_bytes=64)
         for half in range(SLOTS // 2):
             turn_rows(eiw_rows[:], grouped_eiw_t[:], half)
-        first_states("inh")
-        quantise(operand[0]["inh"])
+        quantise(operand[0]["exc"])
         quantise_weight(r_codes["inh"], r_scales["inh"], grouped_eiw_t[:])
         ones = prepare.tile([P, P], BF16)
         nc.gpsimd.memset(ones[:], 1.0)
@@ -360,7 +358,6 @@ def tile_eisnucell_pa_t_kernel(
             if g + 2 < N_GROUPS:
                 loaded[g + 2] = load_group(g + 2)
             if ahead:
-                product[n, "exc"] = row_product(loaded[n], n, "exc")
                 operand[n] = {}
                 factor_t[n] = {}
                 for name in ("x", "exc", "inh"):
@@ -372,11 +369,18 @@ def tile_eisnucell_pa_t_kernel(
                     else:
                         term = row_term[g, pop][i][:]
                     new_state(operand[g], pop, state[pop], i, term)
-                    relu(state[pop], i, not ahead)
                     if not ahead:
+                        relu(state[pop], i, True)
                         store(g, pop, state[pop], i, i + 1)
-                if ahead:
-                    store(g, pop, state[pop], 0, SLOTS)
+                    elif i not in {"exc": [3], "inh": [3]}[pop]:
+                        relu(state[pop], i, False)
+                    if ahead and (pop, i) == ("exc", 0):
+                        for each in POPS:
+                            product[n, each] = row_product(loaded[n], n, each)
+                if ahead and pop == "inh":
+                    for each in POPS:
+                        row_leak(n, each, row_term[n, each], product[n, each])
+                done = state[pop]
                 following = (g, "inh") if pop == "exc" else (n, "exc")
                 if pop == "inh" and not ahead:
                     break
@@ -401,6 +405,10 @@ def tile_eisnucell_pa_t_kernel(
                             operand[n][OTHER[pop]]["grouped"][:],
                             i,
                         )
+                    if ahead and i == 1:
+                        for late in {"exc": [3], "inh": [3]}[pop]:
+                            relu(done, late, True)
+                        store(g, pop, done, 0, SLOTS)
                     if ahead and i >= SLOTS // 2:
                         turn_states(
                             loaded[n]["s_" + pop][:],
@@ -412,7 +420,5 @@ def tile_eisnucell_pa_t_kernel(
                 if ahead:
                     quantise(operand[n]["x" if pop == "exc" else "exc"])
                     if pop == "exc":
-                        row_term[n, "exc"] = row_factors(
-                            loaded[n], n, "exc", product[n, "exc"]
-                        )
-                        row_leak(n, "exc", row_term[n, "exc"], product[n, "exc"])
+                        for each in POPS:
+                            row_term[n, each] = row_factors(loaded[n], n, each, product[n, each])

@@ -24,21 +24,20 @@ LARGEST_F32 = 3.4028234663852886e38
 POPS = ("exc", "inh")
 OTHER = {"exc": "inh", "inh": "exc"}
 SIGN = {"exc": 1.0, "inh": -1.0}
-FIRST_CHUNK = {"exc": 0, "inh": CHUNKS}
+FIRST_UNIT = {"exc": 0, "inh": UNITS}
+SCALAR_RELU_SLOT = SLOTS - 1
 
 FLOPS = 4 * 2 * BATCH * K * UNITS
 
 
 def row_slots(g, pop):
-    return range(SLOTS - row_slot_count(g, pop), SLOTS)
+    if pop == "exc" and g > 0:
+        return [SLOTS - 1]
+    return []
 
 
 def turned_slots(g, pop):
-    return range(SLOTS - row_slot_count(g, pop))
-
-
-def row_slot_count(g, pop):
-    return 0 if g == 0 or pop == "inh" else 1
+    return [i for i in range(SLOTS) if i not in row_slots(g, pop)]
 
 
 def tile_eisnucell_pa_t_kernel(
@@ -69,6 +68,8 @@ def tile_eisnucell_pa_t_kernel(
         tc.psum_pool(name="psum", bufs=PSUM_BANKS) as psum,
         tc.manual_schedule(),
     ):
+        loaded, operand, factor_t, state, product, row_term = {}, {}, {}, {}, {}, {}
+
         identity_f32 = keep.tile([P, P], F32)
         make_identity(nc, identity_f32[:])
 
@@ -77,12 +78,18 @@ def tile_eisnucell_pa_t_kernel(
             nc.sync.dma_start(out=tiles[name][:], in_=inputs[name][g])
 
         def load_group(g):
-            tiles = {}
+            loaded[g] = {}
             for name in ("x", "y_inh", "s_exc", "y_exc", "s_inh"):
-                load_rows(tiles, g, name)
-            return tiles
+                load_rows(loaded[g], g, name)
 
-        def turn_rows(rows, grouped, half, copy=nc.scalar.copy):
+        def load_k_first(raw, weight):
+            for u in range(2):
+                nc.sync.dma_start(
+                    out=raw[:, 2 * u : 2 * u + 2, :],
+                    in_=weight[256 * u : 256 * u + 256, :].rearrange("(p e) n -> p e n", e=2),
+                )
+
+        def turn_rows(rows, grouped, half, copy):
             words = rows.bitcast(F32)
             grouped_words = grouped.bitcast(F32).rearrange("p (i r u) -> p i r u", i=SLOTS, u=2)
             turned = psum.tile([P, 2, 2, P], F32, tag="bank")
@@ -97,180 +104,186 @@ def tile_eisnucell_pa_t_kernel(
                 in_=turned[:].rearrange("p a u r -> p a r u"),
             )
 
-        def new_operand(name):
+        def new_codes(pool, columns, name):
             return {
-                "grouped": packed.tile(
-                    [P, GROUP_ROWS * PACK], BF16, name="grouped_" + name, align_bytes=64
-                ),
-                "codes": packed.tile([P, GROUP_ROWS], U32, name="codes_" + name, align_bytes=64),
-                "scales": packed.tile([P, GROUP_ROWS], U8, name="scales_" + name, align_bytes=64),
+                "codes": pool.tile([P, columns], U32, name="codes_" + name, align_bytes=64),
+                "scales": pool.tile([P, columns], U8, name="scales_" + name, align_bytes=64),
             }
 
-        def quantise(one_operand):
+        def quantise_weight(weight, grouped):
             nc.vector.quantize_mx(
-                out=one_operand["codes"][:].bitcast(FP8X4),
-                scales=one_operand["scales"][:],
-                in_=one_operand["grouped"][:],
+                out=weight["codes"][:].bitcast(FP8X4), scales=weight["scales"][:], in_=grouped
             )
 
-        def turn_states(s_rows, factor_t, pop, pair, slots):
-            words = s_rows.bitcast(F32)
+        def new_operand(g, name):
+            operand[g, name] = new_codes(packed, GROUP_ROWS, name)
+            operand[g, name]["grouped"] = packed.tile(
+                [P, GROUP_ROWS * PACK], BF16, name="grouped_" + name, align_bytes=64
+            )
+
+        def quantise(g, name):
+            quantise_weight(operand[g, name], operand[g, name]["grouped"][:])
+
+        def turn_states(g, pop, u):
+            slots = turned_slots(g, pop)
+            words = loaded[g]["s_" + pop][:].bitcast(F32)
             turned = psum.tile([P, len(slots) * P], F32, tag="bank")
             for i in slots:
-                first = i * WORDS + pair * P
+                first = i * WORDS + u * P
                 nc.tensor.transpose(
                     turned[:, i * P : (i + 1) * P], words[:, first : first + P], identity_f32[:]
                 )
             halves = turned[:].bitcast(BF16).rearrange("p (n e) -> p e n", e=2)
+            if u == 0:
+                factor_t[g, pop] = factors.tile(
+                    [P, CHUNKS, len(slots) * P], F32, name="factor_t_" + pop
+                )
             for e in range(2):
-                column = FIRST_CHUNK[pop] + 2 * pair + e
+                column = CHUNKS * POPS.index(pop) + 2 * u + e
                 nc.scalar.activation(
-                    out=factor_t[:, 2 * e + pair, :],
+                    out=factor_t[g, pop][:, 2 * e + u, :],
                     in_=halves[:, e, :],
                     func=ACT.Identity,
                     bias=1.0,
                     scale=minus_l[:, column : column + 1],
                 )
 
-        def leak_term(factor_t, y_rows, state, i):
+        def leak_term(g, pop, i):
+            if i == 0:
+                state[g, pop] = results.tile([P, SLOTS, UNITS], F32, name="state_" + pop)
             factor = psum.tile([P, UNITS], F32, tag="bank")
             for chunk in range(CHUNKS):
                 nc.tensor.transpose(
                     factor[:, chunk * P : (chunk + 1) * P],
-                    factor_t[:, chunk, i * P : (i + 1) * P],
+                    factor_t[g, pop][:, chunk, i * P : (i + 1) * P],
                     identity_f32[:],
                 )
             nc.vector.scalar_tensor_tensor(
-                out=state[:, i, :].rearrange("p (w e) -> p w e", e=2),
-                in0=y_rows[:, i * UNITS : (i + 1) * UNITS].rearrange("p (w e) -> p w e", e=2),
+                out=state[g, pop][:, i, :].rearrange("p (w e) -> p w e", e=2),
+                in0=loaded[g]["y_" + pop][:, i * UNITS : (i + 1) * UNITS].rearrange(
+                    "p (w e) -> p w e", e=2
+                ),
                 scalar=1.0,
                 in1=factor[:].rearrange("p (e w) -> p w e", e=2),
                 op0=ALU.subtract,
                 op1=ALU.mult,
             )
 
-        def new_factor_t(g, pop):
-            columns = len(turned_slots(g, pop)) * P
-            return factors.tile([P, CHUNKS, columns], F32, name="factor_t_" + pop)
-
-        def row_product(rows, g, pop):
-            first_unit = FIRST_CHUNK[pop] * P
-            product = {}
+        def row_product(g, pop):
             for i in row_slots(g, pop):
-                product[i] = terms.tile([P, UNITS], F32, name="row_factor_%s" % pop)
+                product[g, pop, i] = terms.tile([P, UNITS], F32, name="product_" + pop)
                 nc.gpsimd.tensor_tensor(
-                    out=product[i][:],
-                    in0=rows["s_" + pop][:, i * UNITS : (i + 1) * UNITS],
-                    in1=l_everywhere[:, first_unit : first_unit + UNITS],
+                    out=product[g, pop, i][:],
+                    in0=loaded[g]["s_" + pop][:, i * UNITS : (i + 1) * UNITS],
+                    in1=l_everywhere[:, FIRST_UNIT[pop] : FIRST_UNIT[pop] + UNITS],
                     op=ALU.mult,
                 )
-            return product
 
-        def row_factors(rows, g, pop, product):
-            term = {}
+        def row_factors(g, pop):
             for i in row_slots(g, pop):
+                row_term[g, pop, i] = terms.tile([P, UNITS], F32, name="row_term_" + pop)
                 nc.scalar.activation(
-                    out=product[i][:], in_=product[i][:], func=ACT.Identity, bias=1.0, scale=-1.0
-                )
-                term[i] = terms.tile([P, UNITS], F32, name="row_term_%s" % pop)
-                nc.scalar.activation(
-                    out=term[i][:],
-                    in_=rows["y_" + pop][:, i * UNITS : (i + 1) * UNITS],
+                    out=row_term[g, pop, i][:],
+                    in_=loaded[g]["y_" + pop][:, i * UNITS : (i + 1) * UNITS],
                     func=ACT.Identity,
                     bias=-1.0,
                 )
-            return term
+                nc.scalar.activation(
+                    out=product[g, pop, i][:],
+                    in_=product[g, pop, i][:],
+                    func=ACT.Identity,
+                    bias=1.0,
+                    scale=-1.0,
+                )
 
-        def row_leak(g, pop, term, product):
+        def row_leak(g, pop):
             for i in row_slots(g, pop):
                 nc.gpsimd.tensor_tensor(
-                    out=term[i][:], in0=term[i][:], in1=product[i][:], op=ALU.mult
+                    out=row_term[g, pop, i][:],
+                    in0=row_term[g, pop, i][:],
+                    in1=product[g, pop, i][:],
+                    op=ALU.mult,
                 )
 
-        def new_state(group_operand, pop, state, i, term):
+        def sums(g, pop, i):
             slot = slice(i * P, (i + 1) * P)
             acc = psum.tile([P, UNITS], F32, tag="bank")
-            nc.tensor.matmul_mx(
-                out=acc[:],
-                lhsT=group_operand["x"]["codes"][:, slot].bitcast(FP8X4),
-                lhsT_scale=group_operand["x"]["scales"][:, slot],
-                rhs=w_codes[pop][:].bitcast(FP8X4),
-                rhs_scale=w_scales[pop][:],
-                start=True,
-                stop=False,
-            )
-            nc.tensor.matmul_mx(
-                out=acc[:],
-                lhsT=group_operand[OTHER[pop]]["codes"][:, slot].bitcast(FP8X4),
-                lhsT_scale=group_operand[OTHER[pop]]["scales"][:, slot],
-                rhs=r_codes[pop][:].bitcast(FP8X4),
-                rhs_scale=r_scales[pop][:],
-                start=False,
-                stop=True,
-            )
-            nc.vector.scalar_tensor_tensor(
-                out=state[:, i, :],
-                in0=term,
-                scalar=1.0,
-                in1=acc[:],
-                op0=ALU.add,
-                op1=ALU.add if pop == "exc" else ALU.subtract,
-            )
-
-        def relu(state, i, on_scalar):
-            if on_scalar:
-                nc.scalar.activation(out=state[:, i, :], in_=state[:, i, :], func=ACT.Relu)
-            else:
-                nc.gpsimd.tensor_scalar(
-                    out=state[:, i, :],
-                    in0=state[:, i, :],
-                    scalar1=LARGEST_F32,
-                    scalar2=0.0,
-                    op0=ALU.min,
-                    op1=ALU.max,
+            for name, weight in (("x", w[pop]), (OTHER[pop], r[pop])):
+                nc.tensor.matmul_mx(
+                    out=acc[:],
+                    lhsT=operand[g, name]["codes"][:, slot].bitcast(FP8X4),
+                    lhsT_scale=operand[g, name]["scales"][:, slot],
+                    rhs=weight["codes"][:].bitcast(FP8X4),
+                    rhs_scale=weight["scales"][:],
+                    start=name == "x",
+                    stop=name != "x",
                 )
+            return acc
 
-        def new_result(pop):
-            return results.tile([P, SLOTS, UNITS], F32, name="state_" + pop)
+        def new_state(g, pop, i, acc, columns):
+            if i in row_slots(g, pop):
+                term = row_term[g, pop, i][:]
+            else:
+                term = state[g, pop][:, i, :]
+            nc.vector.scalar_tensor_tensor(
+                out=state[g, pop][:, i, columns],
+                in0=term[:, columns],
+                scalar=1.0,
+                in1=acc[:, columns],
+                op0=ALU.add,
+                op1=ALU.add if SIGN[pop] > 0.0 else ALU.subtract,
+            )
 
-        def store(g, pop, state, first, end):
+        def relu_on_gpsimd(g, pop, i):
+            nc.gpsimd.tensor_scalar(
+                out=state[g, pop][:, i, :],
+                in0=state[g, pop][:, i, :],
+                scalar1=LARGEST_F32,
+                scalar2=0.0,
+                op0=ALU.min,
+                op1=ALU.max,
+            )
+
+        def relu_on_scalar(g, pop, i, columns):
+            nc.scalar.activation(
+                out=state[g, pop][:, i, columns],
+                in_=state[g, pop][:, i, columns],
+                func=ACT.Relu,
+            )
+
+        def store(g, pop, first, end):
             nc.sync.dma_start(
-                out=outputs[pop][g][:, first * UNITS : end * UNITS],
-                in_=state[:, first:end, :].rearrange("p i n -> p (i n)"),
+                out=outputs[pop][g][:, first:end],
+                in_=state[g, pop][:].rearrange("p i n -> p (i n)")[:, first:end],
             )
 
         l_rows = prepare.tile([P, P], F32)
         nc.vector.memset(l_rows[:], 0.0)
         l_row = prepare.tile([P, 2 * UNITS], BF16)
         nc.gpsimd.memset(l_row[:], 0.0)
-        raw_iw = prepare.tile([P, PACK, 2 * UNITS], BF16)
+        ones = prepare.tile([P, P], BF16)
+        nc.gpsimd.memset(ones[:], 1.0)
+        raw_w = {pop: prepare.tile([P, PACK, UNITS], BF16, name="raw_w_" + pop) for pop in POPS}
         raw_eiw = prepare.tile([P, PACK, UNITS], BF16)
         eiw_rows = prepare.tile([P, SLOTS * K], BF16)
-        loaded = {0: {}}
-
-        def load_k_first(raw, weight):
-            for u in range(2):
-                nc.sync.dma_start(
-                    out=raw[:, 2 * u : 2 * u + 2, :],
-                    in_=weight[256 * u : 256 * u + 256, :].rearrange("(p e) n -> p e n", e=2),
-                )
-
-        load_k_first(raw_iw, iw)
+        loaded[0] = {}
+        load_k_first(raw_w["exc"], iw[:, 0:UNITS])
         nc.sync.dma_start(
             out=l_rows[:].bitcast(BF16)[0:CHUNKS, :], in_=l.rearrange("(c k) -> c k", c=CHUNKS)
         )
         load_rows(loaded[0], 0, "s_exc")
+        load_k_first(raw_eiw, eiw)
         load_rows(loaded[0], 0, "x")
         load_rows(loaded[0], 0, "y_exc")
-        load_k_first(raw_eiw, eiw)
         load_rows(loaded[0], 0, "y_inh")
+        load_k_first(raw_w["inh"], iw[:, UNITS : 2 * UNITS])
         load_rows(loaded[0], 0, "s_inh")
         nc.sync.dma_start(
             out=eiw_rows[:].rearrange("p (c k) -> p c k", c=SLOTS),
             in_=eiw.rearrange("(c p) k -> p c k", p=P),
         )
         nc.sync.dma_start(out=l_row[0:1, :], in_=l.rearrange("(a n) -> a n", a=1))
-        loaded[1] = load_group(1)
+        load_group(1)
 
         l_turned = psum.tile([P, P], F32, tag="bank")
         nc.tensor.transpose(l_turned[:], l_rows[:], identity_f32[:])
@@ -279,70 +292,53 @@ def tile_eisnucell_pa_t_kernel(
             out=minus_l[:], in_=l_turned[:].bitcast(BF16)[:, 0 : 2 * CHUNKS], mul=-1.0
         )
 
-        w_codes, w_scales, r_codes, r_scales = {}, {}, {}, {}
-        for pop in POPS:
-            w_codes[pop] = keep.tile([P, UNITS], U32, name="w_codes_" + pop, align_bytes=64)
-            w_scales[pop] = keep.tile([P, UNITS], U8, name="w_scales_" + pop, align_bytes=64)
-            r_codes[pop] = keep.tile([P, UNITS], U32, name="r_codes_" + pop, align_bytes=64)
-            r_scales[pop] = keep.tile([P, UNITS], U8, name="r_scales_" + pop, align_bytes=64)
-
-        def quantise_weight(codes, scales, grouped):
-            nc.vector.quantize_mx(out=codes[:].bitcast(FP8X4), scales=scales[:], in_=grouped)
-
-        def first_operand(name, source, copy=nc.scalar.copy):
-            operand[0][name] = new_operand(name)
-            for half in range(SLOTS // 2):
-                turn_rows(loaded[0][source][:], operand[0][name]["grouped"][:], half, copy)
-
-        def first_states(pop):
-            factor_t[0][pop] = new_factor_t(0, pop)
-            for pair in range(CHUNKS // 2):
-                turn_states(
-                    loaded[0]["s_" + pop][:], factor_t[0][pop], pop, pair, turned_slots(0, pop)
-                )
-
-        operand = {0: {}}
-        factor_t = {0: {}}
-
+        w = {pop: new_codes(keep, UNITS, "w_" + pop) for pop in POPS}
+        r = {pop: new_codes(keep, UNITS, "r_" + pop) for pop in POPS}
         grouped_w = {}
-        for pop in POPS:
-            first_unit = FIRST_CHUNK[pop] * P
+
+        def regroup_w(pop):
             grouped_w[pop] = prepare.tile(
-                [P, UNITS, PACK], BF16, name="grouped_w_" + pop, align_bytes=64
+                [P, UNITS * PACK], BF16, name="grouped_w_" + pop, align_bytes=64
             )
             nc.vector.tensor_scalar_mul(
-                out=grouped_w[pop][:],
-                in0=raw_iw[:, :, first_unit : first_unit + UNITS].rearrange("p t n -> p n t"),
+                out=grouped_w[pop][:].rearrange("p (n t) -> p n t", t=PACK),
+                in0=raw_w[pop][:].rearrange("p t n -> p n t"),
                 scalar1=SIGN[pop],
             )
-        quantise_weight(
-            w_codes["exc"], w_scales["exc"], grouped_w["exc"][:].rearrange("p n t -> p (n t)")
-        )
+
+        def first_operand(name, source, copy):
+            new_operand(0, name)
+            for half in range(SLOTS // 2):
+                turn_rows(
+                    loaded[0][source][:], operand[0, name]["grouped"][:], half, copy
+                )
+
+        def first_states(pop):
+            for u in range(2):
+                turn_states(0, pop, u)
+
+        regroup_w("exc")
+        quantise_weight(w["exc"], grouped_w["exc"][:])
         first_states("exc")
-        first_operand("x", "x", nc.vector.tensor_copy)
-        first_operand("exc", "y_exc")
-        quantise_weight(
-            w_codes["inh"], w_scales["inh"], grouped_w["inh"][:].rearrange("p n t -> p (n t)")
-        )
-        quantise(operand[0]["x"])
-        state = {"exc": new_result("exc")}
-        for i in turned_slots(0, "exc"):
-            leak_term(factor_t[0]["exc"], loaded[0]["y_exc"], state["exc"], i)
         grouped_eiw = prepare.tile([P, UNITS, PACK], BF16, align_bytes=64)
         nc.vector.tensor_copy(out=grouped_eiw[:], in_=raw_eiw[:].rearrange("p t n -> p n t"))
-        quantise_weight(
-            r_codes["exc"], r_scales["exc"], grouped_eiw[:].rearrange("p n t -> p (n t)")
-        )
-        first_operand("inh", "y_inh")
-        quantise(operand[0]["inh"])
+        quantise_weight(r["exc"], grouped_eiw[:].rearrange("p n t -> p (n t)"))
+        first_operand("x", "x", nc.vector.tensor_copy)
+        quantise(0, "x")
+        first_operand("exc", "y_exc", nc.scalar.copy)
+        for i in turned_slots(0, "exc"):
+            leak_term(0, "exc", i)
+        first_operand("inh", "y_inh", nc.scalar.copy)
+        quantise(0, "inh")
+        regroup_w("inh")
         first_states("inh")
         grouped_eiw_t = prepare.tile([P, UNITS * PACK], BF16, align_bytes=64)
         for half in range(SLOTS // 2):
-            turn_rows(eiw_rows[:], grouped_eiw_t[:], half)
-        quantise(operand[0]["exc"])
-        quantise_weight(r_codes["inh"], r_scales["inh"], grouped_eiw_t[:])
-        ones = prepare.tile([P, P], BF16)
-        nc.gpsimd.memset(ones[:], 1.0)
+            turn_rows(eiw_rows[:], grouped_eiw_t[:], half, nc.scalar.copy)
+        quantise_weight(w["inh"], grouped_w["inh"][:])
+        quantise(0, "exc")
+        quantise_weight(r["inh"], grouped_eiw_t[:])
+
         l_everywhere = keep.tile([P, 2 * UNITS], BF16)
         for half in range(2):
             columns = slice(half * UNITS, (half + 1) * UNITS)
@@ -350,75 +346,54 @@ def tile_eisnucell_pa_t_kernel(
             nc.tensor.matmul(spread[:], ones[:], l_row[:, columns], start=True, stop=True)
             nc.scalar.copy(out=l_everywhere[:, columns], in_=spread[:])
 
-        product, row_term = {}, {}
-
+        whole = slice(0, UNITS)
         for g in range(N_GROUPS):
             n = g + 1
             ahead = n < N_GROUPS
             if g + 2 < N_GROUPS:
-                loaded[g + 2] = load_group(g + 2)
+                load_group(g + 2)
             if ahead:
-                operand[n] = {}
-                factor_t[n] = {}
                 for name in ("x", "exc", "inh"):
-                    operand[n][name] = new_operand(name)
+                    new_operand(n, name)
             for pop in POPS:
                 for i in range(SLOTS):
-                    if i in turned_slots(g, pop):
-                        term = state[pop][:, i, :]
-                    else:
-                        term = row_term[g, pop][i][:]
-                    new_state(operand[g], pop, state[pop], i, term)
-                    if not ahead:
-                        relu(state[pop], i, True)
-                        store(g, pop, state[pop], i, i + 1)
-                    elif i not in {"exc": [3], "inh": [3]}[pop]:
-                        relu(state[pop], i, False)
+                    acc = sums(g, pop, i)
+                    last = not ahead and pop == "inh" and i == SLOTS - 1
+                    pieces = [slice(0, UNITS // 2), slice(UNITS // 2, UNITS)] if last else [whole]
+                    for columns in pieces:
+                        new_state(g, pop, i, acc, columns)
+                        if not ahead:
+                            relu_on_scalar(g, pop, i, columns)
+                            store(g, pop, i * UNITS + columns.start, i * UNITS + columns.stop)
+                    if g > 0 and (pop, i) == ("exc", 0):
+                        quantise(g, "exc")
+                    if ahead and i != SCALAR_RELU_SLOT:
+                        relu_on_gpsimd(g, pop, i)
                     if ahead and (pop, i) == ("exc", 0):
-                        for each in POPS:
-                            product[n, each] = row_product(loaded[n], n, each)
+                        row_product(n, "exc")
                 if ahead and pop == "inh":
-                    for each in POPS:
-                        row_leak(n, each, row_term[n, each], product[n, each])
-                done = state[pop]
-                following = (g, "inh") if pop == "exc" else (n, "exc")
-                if pop == "inh" and not ahead:
-                    break
-                state[following[1]] = new_result(following[1])
-                if ahead:
-                    factor_t[n][pop] = new_factor_t(n, pop)
-                    if pop == "inh":
-                        quantise(operand[n]["inh"])
+                    row_leak(n, "exc")
+                    quantise(n, "inh")
+                turned = (g, "inh") if pop == "exc" else (n, "exc")
                 for i in range(SLOTS):
-                    if i in turned_slots(*following):
-                        leak_term(
-                            factor_t[following[0]][following[1]],
-                            loaded[following[0]]["y_" + following[1]],
-                            state[following[1]],
-                            i,
-                        )
-                    if ahead and pop == "exc" and i < SLOTS // 2:
-                        turn_rows(loaded[n]["x"][:], operand[n]["x"]["grouped"][:], i)
+                    if turned[0] < N_GROUPS and i in turned_slots(*turned):
+                        leak_term(*turned, i)
                     if ahead and i < SLOTS // 2:
+                        if pop == "exc":
+                            turn_rows(
+                                loaded[n]["x"][:], operand[n, "x"]["grouped"][:], i, nc.scalar.copy
+                            )
                         turn_rows(
                             loaded[n]["y_" + OTHER[pop]][:],
-                            operand[n][OTHER[pop]]["grouped"][:],
+                            operand[n, OTHER[pop]]["grouped"][:],
                             i,
+                            nc.scalar.copy,
                         )
                     if ahead and i == 1:
-                        for late in {"exc": [3], "inh": [3]}[pop]:
-                            relu(done, late, True)
-                        store(g, pop, done, 0, SLOTS)
+                        relu_on_scalar(g, pop, SCALAR_RELU_SLOT, whole)
+                        store(g, pop, 0, SLOTS * UNITS)
                     if ahead and i >= SLOTS // 2:
-                        turn_states(
-                            loaded[n]["s_" + pop][:],
-                            factor_t[n][pop],
-                            pop,
-                            i - SLOTS // 2,
-                            turned_slots(n, pop),
-                        )
-                if ahead:
-                    quantise(operand[n]["x" if pop == "exc" else "exc"])
-                    if pop == "exc":
-                        for each in POPS:
-                            row_term[n, each] = row_factors(loaded[n], n, each, product[n, each])
+                        turn_states(n, pop, i - SLOTS // 2)
+                if ahead and pop == "exc":
+                    quantise(n, "x")
+                    row_factors(n, "exc")

@@ -25,7 +25,7 @@ POPS = ("exc", "inh")
 OTHER = {"exc": "inh", "inh": "exc"}
 SIGN = {"exc": 1.0, "inh": -1.0}
 FIRST_UNIT = {"exc": 0, "inh": UNITS}
-SCALAR_RELU_SLOT = SLOTS - 1
+SCALAR_RELU = {"exc": [3], "inh": [3]}
 
 FLOPS = 4 * 2 * BATCH * K * UNITS
 
@@ -106,8 +106,8 @@ def tile_eisnucell_pa_t_kernel(
 
         def new_codes(pool, columns, name):
             return {
-                "codes": pool.tile([P, columns], U32, name="codes_" + name, align_bytes=64),
-                "scales": pool.tile([P, columns], U8, name="scales_" + name, align_bytes=64),
+                "codes": pool.tile([P, columns], U32, name="codes_" + name, align_bytes=256),
+                "scales": pool.tile([P, columns], U8, name="scales_" + name, align_bytes=256),
             }
 
         def quantise_weight(weight, grouped):
@@ -118,7 +118,7 @@ def tile_eisnucell_pa_t_kernel(
         def new_operand(g, name):
             operand[g, name] = new_codes(packed, GROUP_ROWS, name)
             operand[g, name]["grouped"] = packed.tile(
-                [P, GROUP_ROWS * PACK], BF16, name="grouped_" + name, align_bytes=64
+                [P, GROUP_ROWS * PACK], BF16, name="grouped_" + name, align_bytes=256
             )
 
         def quantise(g, name):
@@ -263,20 +263,19 @@ def tile_eisnucell_pa_t_kernel(
         nc.gpsimd.memset(l_row[:], 0.0)
         ones = prepare.tile([P, P], BF16)
         nc.gpsimd.memset(ones[:], 1.0)
-        raw_w = {pop: prepare.tile([P, PACK, UNITS], BF16, name="raw_w_" + pop) for pop in POPS}
+        raw_iw = prepare.tile([P, PACK, 2 * UNITS], BF16)
         raw_eiw = prepare.tile([P, PACK, UNITS], BF16)
         eiw_rows = prepare.tile([P, SLOTS * K], BF16)
         loaded[0] = {}
-        load_k_first(raw_w["exc"], iw[:, 0:UNITS])
+        load_k_first(raw_iw, iw)
         nc.sync.dma_start(
             out=l_rows[:].bitcast(BF16)[0:CHUNKS, :], in_=l.rearrange("(c k) -> c k", c=CHUNKS)
         )
         load_rows(loaded[0], 0, "s_exc")
-        load_k_first(raw_eiw, eiw)
         load_rows(loaded[0], 0, "x")
         load_rows(loaded[0], 0, "y_exc")
+        load_k_first(raw_eiw, eiw)
         load_rows(loaded[0], 0, "y_inh")
-        load_k_first(raw_w["inh"], iw[:, UNITS : 2 * UNITS])
         load_rows(loaded[0], 0, "s_inh")
         nc.sync.dma_start(
             out=eiw_rows[:].rearrange("p (c k) -> p c k", c=SLOTS),
@@ -298,11 +297,13 @@ def tile_eisnucell_pa_t_kernel(
 
         def regroup_w(pop):
             grouped_w[pop] = prepare.tile(
-                [P, UNITS * PACK], BF16, name="grouped_w_" + pop, align_bytes=64
+                [P, UNITS * PACK], BF16, name="grouped_w_" + pop, align_bytes=256
             )
             nc.vector.tensor_scalar_mul(
                 out=grouped_w[pop][:].rearrange("p (n t) -> p n t", t=PACK),
-                in0=raw_w[pop][:].rearrange("p t n -> p n t"),
+                in0=raw_iw[:, :, FIRST_UNIT[pop] : FIRST_UNIT[pop] + UNITS].rearrange(
+                    "p t n -> p n t"
+                ),
                 scalar1=SIGN[pop],
             )
 
@@ -318,24 +319,24 @@ def tile_eisnucell_pa_t_kernel(
                 turn_states(0, pop, u)
 
         regroup_w("exc")
+        regroup_w("inh")
         quantise_weight(w["exc"], grouped_w["exc"][:])
         first_states("exc")
-        grouped_eiw = prepare.tile([P, UNITS, PACK], BF16, align_bytes=64)
-        nc.vector.tensor_copy(out=grouped_eiw[:], in_=raw_eiw[:].rearrange("p t n -> p n t"))
-        quantise_weight(r["exc"], grouped_eiw[:].rearrange("p n t -> p (n t)"))
         first_operand("x", "x", nc.vector.tensor_copy)
-        quantise(0, "x")
         first_operand("exc", "y_exc", nc.scalar.copy)
+        quantise_weight(w["inh"], grouped_w["inh"][:])
+        quantise(0, "x")
         for i in turned_slots(0, "exc"):
             leak_term(0, "exc", i)
+        grouped_eiw = prepare.tile([P, UNITS, PACK], BF16, align_bytes=256)
+        nc.vector.tensor_copy(out=grouped_eiw[:], in_=raw_eiw[:].rearrange("p t n -> p n t"))
+        quantise_weight(r["exc"], grouped_eiw[:].rearrange("p n t -> p (n t)"))
         first_operand("inh", "y_inh", nc.scalar.copy)
         quantise(0, "inh")
-        regroup_w("inh")
         first_states("inh")
-        grouped_eiw_t = prepare.tile([P, UNITS * PACK], BF16, align_bytes=64)
+        grouped_eiw_t = prepare.tile([P, UNITS * PACK], BF16, align_bytes=256)
         for half in range(SLOTS // 2):
             turn_rows(eiw_rows[:], grouped_eiw_t[:], half, nc.scalar.copy)
-        quantise_weight(w["inh"], grouped_w["inh"][:])
         quantise(0, "exc")
         quantise_weight(r["inh"], grouped_eiw_t[:])
 
@@ -345,6 +346,18 @@ def tile_eisnucell_pa_t_kernel(
             spread = psum.tile([P, UNITS], F32, tag="bank")
             nc.tensor.matmul(spread[:], ones[:], l_row[:, columns], start=True, stop=True)
             nc.scalar.copy(out=l_everywhere[:, columns], in_=spread[:])
+
+        def leak(g, pop, i):
+            if i in turned_slots(g, pop):
+                leak_term(g, pop, i)
+
+        def turn(g, name, source, half):
+            turn_rows(loaded[g][source][:], operand[g, name]["grouped"][:], half, nc.scalar.copy)
+
+        def late_relus(g, pop):
+            for i in SCALAR_RELU[pop]:
+                relu_on_scalar(g, pop, i, whole)
+            store(g, pop, 0, SLOTS * UNITS)
 
         whole = slice(0, UNITS)
         for g in range(N_GROUPS):
@@ -356,44 +369,45 @@ def tile_eisnucell_pa_t_kernel(
                 for name in ("x", "exc", "inh"):
                     new_operand(n, name)
             for pop in POPS:
+                turned = (g, "inh") if pop == "exc" else (n, "exc")
                 for i in range(SLOTS):
                     acc = sums(g, pop, i)
-                    last = not ahead and pop == "inh" and i == SLOTS - 1
-                    pieces = [slice(0, UNITS // 2), slice(UNITS // 2, UNITS)] if last else [whole]
-                    for columns in pieces:
-                        new_state(g, pop, i, acc, columns)
-                        if not ahead:
-                            relu_on_scalar(g, pop, i, columns)
-                            store(g, pop, i * UNITS + columns.start, i * UNITS + columns.stop)
+                    new_state(g, pop, i, acc, whole)
+                    if not ahead:
+                        relu_on_scalar(g, pop, i, whole)
+                        store(g, pop, i * UNITS, (i + 1) * UNITS)
                     if g > 0 and (pop, i) == ("exc", 0):
                         quantise(g, "exc")
-                    if ahead and i != SCALAR_RELU_SLOT:
+                    if ahead and i not in SCALAR_RELU[pop]:
                         relu_on_gpsimd(g, pop, i)
                     if ahead and (pop, i) == ("exc", 0):
                         row_product(n, "exc")
-                if ahead and pop == "inh":
-                    row_leak(n, "exc")
-                    quantise(n, "inh")
-                turned = (g, "inh") if pop == "exc" else (n, "exc")
-                for i in range(SLOTS):
-                    if turned[0] < N_GROUPS and i in turned_slots(*turned):
-                        leak_term(*turned, i)
-                    if ahead and i < SLOTS // 2:
-                        if pop == "exc":
-                            turn_rows(
-                                loaded[n]["x"][:], operand[n, "x"]["grouped"][:], i, nc.scalar.copy
-                            )
-                        turn_rows(
-                            loaded[n]["y_" + OTHER[pop]][:],
-                            operand[n, OTHER[pop]]["grouped"][:],
-                            i,
-                            nc.scalar.copy,
-                        )
-                    if ahead and i == 1:
-                        relu_on_scalar(g, pop, SCALAR_RELU_SLOT, whole)
-                        store(g, pop, 0, SLOTS * UNITS)
-                    if ahead and i >= SLOTS // 2:
-                        turn_states(n, pop, i - SLOTS // 2)
                 if ahead and pop == "exc":
+                    leak(*turned, 0)
+                    turn(n, "x", "x", 0)
+                    turn(n, "inh", "y_inh", 0)
+                    leak(*turned, 1)
+                    turn(n, "x", "x", 1)
+                    turn(n, "inh", "y_inh", 1)
+                    leak(*turned, 2)
+                    turn_states(n, pop, 0)
+                    leak(*turned, 3)
+                    turn_states(n, pop, 1)
+                    late_relus(g, pop)
                     quantise(n, "x")
                     row_factors(n, "exc")
+                elif ahead:
+                    row_leak(n, "exc")
+                    quantise(n, "inh")
+                    leak(*turned, 0)
+                    turn(n, "exc", "y_exc", 0)
+                    leak(*turned, 1)
+                    turn(n, "exc", "y_exc", 1)
+                    leak(*turned, 2)
+                    turn_states(n, pop, 0)
+                    leak(*turned, 3)
+                    turn_states(n, pop, 1)
+                    late_relus(g, pop)
+                elif pop == "exc":
+                    for i in range(SLOTS):
+                        leak(g, "inh", i)

@@ -27,11 +27,14 @@ SIGN = {"exc": 1.0, "inh": -1.0}
 FIRST_UNIT = {"exc": 0, "inh": UNITS}
 SCALAR_RELU = {"exc": [3], "inh": [3]}
 
+LIFTED = (("exc", 0),)
 FLOPS = 4 * 2 * BATCH * K * UNITS
 
 
 def row_slots(g, pop):
     if pop == "exc" and g > 0:
+        return [SLOTS - 1]
+    if pop == "inh" and g == N_GROUPS - 1:
         return [SLOTS - 1]
     return []
 
@@ -220,11 +223,13 @@ def tile_eisnucell_pa_t_kernel(
                 )
             return acc
 
-        def new_state(g, pop, i, acc, columns):
+        def leak_of(g, pop, i):
             if i in row_slots(g, pop):
-                term = row_term[g, pop, i][:]
-            else:
-                term = state[g, pop][:, i, :]
+                return row_term[g, pop, i][:]
+            return state[g, pop][:, i, :]
+
+        def new_state(g, pop, i, acc, columns):
+            term = leak_of(g, pop, i)
             nc.vector.scalar_tensor_tensor(
                 out=state[g, pop][:, i, columns],
                 in0=term[:, columns],
@@ -232,6 +237,15 @@ def tile_eisnucell_pa_t_kernel(
                 in1=acc[:, columns],
                 op0=ALU.add,
                 op1=ALU.add if SIGN[pop] > 0.0 else ALU.subtract,
+            )
+
+        def new_state_off_vector(g, pop, i, acc):
+            lifted = terms.tile([P, UNITS], F32, name="lifted")
+            nc.scalar.activation(
+                out=lifted[:], in_=acc[:], func=ACT.Identity, bias=1.0, scale=SIGN[pop]
+            )
+            nc.gpsimd.tensor_tensor(
+                out=state[g, pop][:, i, :], in0=lifted[:], in1=leak_of(g, pop, i), op=ALU.add
             )
 
         def relu_on_gpsimd(g, pop, i):
@@ -372,10 +386,21 @@ def tile_eisnucell_pa_t_kernel(
                 turned = (g, "inh") if pop == "exc" else (n, "exc")
                 for i in range(SLOTS):
                     acc = sums(g, pop, i)
-                    new_state(g, pop, i, acc, whole)
-                    if not ahead:
+                    lifted = not ahead and (pop, i) in LIFTED
+                    if lifted:
+                        new_state_off_vector(g, pop, i, acc)
+                        relu_on_gpsimd(g, pop, i)
+                    else:
+                        new_state(g, pop, i, acc, whole)
+                    if not ahead and not lifted:
                         relu_on_scalar(g, pop, i, whole)
                         store(g, pop, i * UNITS, (i + 1) * UNITS)
+                    if not ahead and (pop, i) == ("exc", 0):
+                        row_factors(g, "inh")
+                        row_leak(g, "inh")
+                    if not ahead and (pop, i) == ("inh", 1):
+                        for late_pop, late in LIFTED:
+                            store(g, late_pop, late * UNITS, (late + 1) * UNITS)
                     if g > 0 and (pop, i) == ("exc", 0):
                         quantise(g, "exc")
                     if ahead and i not in SCALAR_RELU[pop]:
@@ -398,6 +423,7 @@ def tile_eisnucell_pa_t_kernel(
                     row_factors(n, "exc")
                 elif ahead:
                     row_leak(n, "exc")
+                    row_product(n, "inh")
                     quantise(n, "inh")
                     leak(*turned, 0)
                     turn(n, "exc", "y_exc", 0)

import concourse.mybir as mybir
from concourse.masks import make_identity

FP8X4 = mybir.dt.float8_e4m3fn_x4
BF16 = mybir.dt.bfloat16
F32 = mybir.dt.float32
U32 = mybir.dt.uint32
U8 = mybir.dt.uint8
ALU = mybir.AluOpType
ACT = mybir.ActivationFunctionType

P = 128
PACK = 4
BATCH = 4096
K = 512
UNITS = 512
CHUNKS = UNITS // P
SLOTS = 4
GROUP_ROWS = P * SLOTS
N_GROUPS = BATCH // GROUP_ROWS
WORDS = K // 2
PSUM_BANKS = 8
LARGEST_F32 = 3.4028234663852886e38
POPS = ("exc", "inh")
OTHER = {"exc": "inh", "inh": "exc"}
SIGN = {"exc": 1.0, "inh": -1.0}
FIRST_UNIT = {"exc": 0, "inh": UNITS}
SCALAR_RELU = {"exc": [3], "inh": [3]}

LIFTED = (("exc", 0),)
FLOPS = 4 * 2 * BATCH * K * UNITS


def row_slots(g, pop):
    if pop == "exc" and g > 0:
        return [SLOTS - 1]
    if pop == "inh" and g == N_GROUPS - 1:
        return [SLOTS - 1]
    return []


def turned_slots(g, pop):
    return [i for i in range(SLOTS) if i not in row_slots(g, pop)]


def tile_eisnucell_pa_t_kernel(
    tc, x_t, y_exc, s_exc, y_inh, s_inh, iw, eiw, l, out_0, out_1
):
    nc = tc.nc

    def grouped_view(dram):
        return dram.rearrange("(g p i) c -> g p (i c)", p=P, i=SLOTS)

    inputs = {
        "x": grouped_view(x_t),
        "y_exc": grouped_view(y_exc),
        "y_inh": grouped_view(y_inh),
        "s_exc": grouped_view(s_exc),
        "s_inh": grouped_view(s_inh),
    }
    outputs = {"exc": grouped_view(out_0), "inh": grouped_view(out_1)}

    with (
        tc.tile_pool(name="keep", bufs=1) as keep,
        tc.tile_pool(name="prepare", bufs=1) as prepare,
        tc.tile_pool(name="loads", bufs=3) as loads,
        tc.tile_pool(name="packed", bufs=2) as packed,
        tc.tile_pool(name="factors", bufs=2) as factors,
        tc.tile_pool(name="results", bufs=2) as results,
        tc.tile_pool(name="terms", bufs=2) as terms,
        tc.psum_pool(name="psum", bufs=PSUM_BANKS) as psum,
        tc.manual_schedule(),
    ):
        loaded, operand, factor_t, state, product, row_term = {}, {}, {}, {}, {}, {}

        identity_f32 = keep.tile([P, P], F32)
        make_identity(nc, identity_f32[:])

        def load_rows(tiles, g, name):
            tiles[name] = loads.tile([P, SLOTS * K], BF16, name="rows_" + name)
            nc.sync.dma_start(out=tiles[name][:], in_=inputs[name][g])

        def load_group(g):
            loaded[g] = {}
            for name in ("x", "y_inh", "s_exc", "y_exc", "s_inh"):
                load_rows(loaded[g], g, name)

        def load_k_first(raw, weight):
            for u in range(2):
                nc.sync.dma_start(
                    out=raw[:, 2 * u : 2 * u + 2, :],
                    in_=weight[256 * u : 256 * u + 256, :].rearrange("(p e) n -> p e n", e=2),
                )

        def turn_rows(rows, grouped, half, copy):
            words = rows.bitcast(F32)
            grouped_words = grouped.bitcast(F32).rearrange("p (i r u) -> p i r u", i=SLOTS, u=2)
            turned = psum.tile([P, 2, 2, P], F32, tag="bank")
            for a in range(2):
                for u in range(2):
                    first = (2 * half + a) * WORDS + u * P
                    nc.tensor.transpose(
                        turned[:, a, u, :], words[:, first : first + P], identity_f32[:]
                    )
            copy(
                out=grouped_words[:, 2 * half : 2 * half + 2, :, :],
                in_=turned[:].rearrange("p a u r -> p a r u"),
            )

        def new_codes(pool, columns, name):
            return {
                "codes": pool.tile([P, columns], U32, name="codes_" + name, align_bytes=256),
                "scales": pool.tile([P, columns], U8, name="scales_" + name, align_bytes=256),
            }

        def quantise_weight(weight, grouped):
            nc.vector.quantize_mx(
                out=weight["codes"][:].bitcast(FP8X4), scales=weight["scales"][:], in_=grouped
            )

        def new_operand(g, name):
            operand[g, name] = new_codes(packed, GROUP_ROWS, name)
            operand[g, name]["grouped"] = packed.tile(
                [P, GROUP_ROWS * PACK], BF16, name="grouped_" + name, align_bytes=256
            )

        def quantise(g, name):
            quantise_weight(operand[g, name], operand[g, name]["grouped"][:])

        def turn_states(g, pop, u):
            slots = turned_slots(g, pop)
            words = loaded[g]["s_" + pop][:].bitcast(F32)
            turned = psum.tile([P, len(slots) * P], F32, tag="bank")
            for i in slots:
                first = i * WORDS + u * P
                nc.tensor.transpose(
                    turned[:, i * P : (i + 1) * P], words[:, first : first + P], identity_f32[:]
                )
            halves = turned[:].bitcast(BF16).rearrange("p (n e) -> p e n", e=2)
            if u == 0:
                factor_t[g, pop] = factors.tile(
                    [P, CHUNKS, len(slots) * P], F32, name="factor_t_" + pop
                )
            for e in range(2):
                column = CHUNKS * POPS.index(pop) + 2 * u + e
                nc.scalar.activation(
                    out=factor_t[g, pop][:, 2 * e + u, :],
                    in_=halves[:, e, :],
                    func=ACT.Identity,
                    bias=1.0,
                    scale=minus_l[:, column : column + 1],
                )

        def leak_term(g, pop, i):
            if i == 0:
                state[g, pop] = results.tile([P, SLOTS, UNITS], F32, name="state_" + pop)
            factor = psum.tile([P, UNITS], F32, tag="bank")
            for chunk in range(CHUNKS):
                nc.tensor.transpose(
                    factor[:, chunk * P : (chunk + 1) * P],
                    factor_t[g, pop][:, chunk, i * P : (i + 1) * P],
                    identity_f32[:],
                )
            nc.vector.scalar_tensor_tensor(
                out=state[g, pop][:, i, :].rearrange("p (w e) -> p w e", e=2),
                in0=loaded[g]["y_" + pop][:, i * UNITS : (i + 1) * UNITS].rearrange(
                    "p (w e) -> p w e", e=2
                ),
                scalar=1.0,
                in1=factor[:].rearrange("p (e w) -> p w e", e=2),
                op0=ALU.subtract,
                op1=ALU.mult,
            )

        def row_product(g, pop):
            for i in row_slots(g, pop):
                product[g, pop, i] = terms.tile([P, UNITS], F32, name="product_" + pop)
                nc.gpsimd.tensor_tensor(
                    out=product[g, pop, i][:],
                    in0=loaded[g]["s_" + pop][:, i * UNITS : (i + 1) * UNITS],
                    in1=l_everywhere[:, FIRST_UNIT[pop] : FIRST_UNIT[pop] + UNITS],
                    op=ALU.mult,
                )

        def row_factors(g, pop):
            for i in row_slots(g, pop):
                row_term[g, pop, i] = terms.tile([P, UNITS], F32, name="row_term_" + pop)
                nc.scalar.activation(
                    out=row_term[g, pop, i][:],
                    in_=loaded[g]["y_" + pop][:, i * UNITS : (i + 1) * UNITS],
                    func=ACT.Identity,
                    bias=-1.0,
                )
                nc.scalar.activation(
                    out=product[g, pop, i][:],
                    in_=product[g, pop, i][:],
                    func=ACT.Identity,
                    bias=1.0,
                    scale=-1.0,
                )

        def row_leak(g, pop):
            for i in row_slots(g, pop):
                nc.gpsimd.tensor_tensor(
                    out=row_term[g, pop, i][:],
                    in0=row_term[g, pop, i][:],
                    in1=product[g, pop, i][:],
                    op=ALU.mult,
                )

        def sums(g, pop, i):
            slot = slice(i * P, (i + 1) * P)
            acc = psum.tile([P, UNITS], F32, tag="bank")
            for name, weight in (("x", w[pop]), (OTHER[pop], r[pop])):
                nc.tensor.matmul_mx(
                    out=acc[:],
                    lhsT=operand[g, name]["codes"][:, slot].bitcast(FP8X4),
                    lhsT_scale=operand[g, name]["scales"][:, slot],
                    rhs=weight["codes"][:].bitcast(FP8X4),
                    rhs_scale=weight["scales"][:],
                    start=name == "x",
                    stop=name != "x",
                )
            return acc

        def leak_of(g, pop, i):
            if i in row_slots(g, pop):
                return row_term[g, pop, i][:]
            return state[g, pop][:, i, :]

        def new_state(g, pop, i, acc, columns):
            term = leak_of(g, pop, i)
            nc.vector.scalar_tensor_tensor(
                out=state[g, pop][:, i, columns],
                in0=term[:, columns],
                scalar=1.0,
                in1=acc[:, columns],
                op0=ALU.add,
                op1=ALU.add if SIGN[pop] > 0.0 else ALU.subtract,
            )

        def new_state_off_vector(g, pop, i, acc):
            lifted = terms.tile([P, UNITS], F32, name="lifted")
            nc.scalar.activation(
                out=lifted[:], in_=acc[:], func=ACT.Identity, bias=1.0, scale=SIGN[pop]
            )
            nc.gpsimd.tensor_tensor(
                out=state[g, pop][:, i, :], in0=lifted[:], in1=leak_of(g, pop, i), op=ALU.add
            )

        def relu_on_gpsimd(g, pop, i):
            nc.gpsimd.tensor_scalar(
                out=state[g, pop][:, i, :],
                in0=state[g, pop][:, i, :],
                scalar1=LARGEST_F32,
                scalar2=0.0,
                op0=ALU.min,
                op1=ALU.max,
            )

        def relu_on_scalar(g, pop, i, columns):
            nc.scalar.activation(
                out=state[g, pop][:, i, columns],
                in_=state[g, pop][:, i, columns],
                func=ACT.Relu,
            )

        def store(g, pop, first, end):
            nc.sync.dma_start(
                out=outputs[pop][g][:, first:end],
                in_=state[g, pop][:].rearrange("p i n -> p (i n)")[:, first:end],
            )

        l_rows = prepare.tile([P, P], F32)
        nc.vector.memset(l_rows[:], 0.0)
        l_row = prepare.tile([P, 2 * UNITS], BF16)
        nc.gpsimd.memset(l_row[:], 0.0)
        ones = prepare.tile([P, P], BF16)
        nc.gpsimd.memset(ones[:], 1.0)
        raw_iw = prepare.tile([P, PACK, 2 * UNITS], BF16)
        raw_eiw = prepare.tile([P, PACK, UNITS], BF16)
        eiw_rows = prepare.tile([P, SLOTS * K], BF16)
        loaded[0] = {}
        load_k_first(raw_iw, iw)
        nc.sync.dma_start(
            out=l_rows[:].bitcast(BF16)[0:CHUNKS, :], in_=l.rearrange("(c k) -> c k", c=CHUNKS)
        )
        load_rows(loaded[0], 0, "s_exc")
        load_rows(loaded[0], 0, "x")
        load_rows(loaded[0], 0, "y_exc")
        load_k_first(raw_eiw, eiw)
        load_rows(loaded[0], 0, "y_inh")
        load_rows(loaded[0], 0, "s_inh")
        nc.sync.dma_start(
            out=eiw_rows[:].rearrange("p (c k) -> p c k", c=SLOTS),
            in_=eiw.rearrange("(c p) k -> p c k", p=P),
        )
        nc.sync.dma_start(out=l_row[0:1, :], in_=l.rearrange("(a n) -> a n", a=1))
        load_group(1)

        l_turned = psum.tile([P, P], F32, tag="bank")
        nc.tensor.transpose(l_turned[:], l_rows[:], identity_f32[:])
        minus_l = keep.tile([P, 2 * CHUNKS], F32)
        nc.scalar.mul(
            out=minus_l[:], in_=l_turned[:].bitcast(BF16)[:, 0 : 2 * CHUNKS], mul=-1.0
        )

        w = {pop: new_codes(keep, UNITS, "w_" + pop) for pop in POPS}
        r = {pop: new_codes(keep, UNITS, "r_" + pop) for pop in POPS}
        grouped_w = {}

        def regroup_w(pop):
            grouped_w[pop] = prepare.tile(
                [P, UNITS * PACK], BF16, name="grouped_w_" + pop, align_bytes=256
            )
            nc.vector.tensor_scalar_mul(
                out=grouped_w[pop][:].rearrange("p (n t) -> p n t", t=PACK),
                in0=raw_iw[:, :, FIRST_UNIT[pop] : FIRST_UNIT[pop] + UNITS].rearrange(
                    "p t n -> p n t"
                ),
                scalar1=SIGN[pop],
            )

        def first_operand(name, source, copy):
            new_operand(0, name)
            for half in range(SLOTS // 2):
                turn_rows(
                    loaded[0][source][:], operand[0, name]["grouped"][:], half, copy
                )

        def first_states(pop):
            for u in range(2):
                turn_states(0, pop, u)

        regroup_w("exc")
        regroup_w("inh")
        quantise_weight(w["exc"], grouped_w["exc"][:])
        first_states("exc")
        first_operand("x", "x", nc.vector.tensor_copy)
        first_operand("exc", "y_exc", nc.scalar.copy)
        quantise_weight(w["inh"], grouped_w["inh"][:])
        quantise(0, "x")
        for i in turned_slots(0, "exc"):
            leak_term(0, "exc", i)
        grouped_eiw = prepare.tile([P, UNITS, PACK], BF16, align_bytes=256)
        nc.vector.tensor_copy(out=grouped_eiw[:], in_=raw_eiw[:].rearrange("p t n -> p n t"))
        quantise_weight(r["exc"], grouped_eiw[:].rearrange("p n t -> p (n t)"))
        first_operand("inh", "y_inh", nc.scalar.copy)
        quantise(0, "inh")
        first_states("inh")
        grouped_eiw_t = prepare.tile([P, UNITS * PACK], BF16, align_bytes=256)
        for half in range(SLOTS // 2):
            turn_rows(eiw_rows[:], grouped_eiw_t[:], half, nc.scalar.copy)
        quantise(0, "exc")
        quantise_weight(r["inh"], grouped_eiw_t[:])

        l_everywhere = keep.tile([P, 2 * UNITS], BF16)
        for half in range(2):
            columns = slice(half * UNITS, (half + 1) * UNITS)
            spread = psum.tile([P, UNITS], F32, tag="bank")
            nc.tensor.matmul(spread[:], ones[:], l_row[:, columns], start=True, stop=True)
            nc.scalar.copy(out=l_everywhere[:, columns], in_=spread[:])

        def leak(g, pop, i):
            if i in turned_slots(g, pop):
                leak_term(g, pop, i)

        def turn(g, name, source, half):
            turn_rows(loaded[g][source][:], operand[g, name]["grouped"][:], half, nc.scalar.copy)

        def late_relus(g, pop):
            for i in SCALAR_RELU[pop]:
                relu_on_scalar(g, pop, i, whole)
            store(g, pop, 0, SLOTS * UNITS)

        whole = slice(0, UNITS)
        for g in range(N_GROUPS):
            n = g + 1
            ahead = n < N_GROUPS
            if g + 2 < N_GROUPS:
                load_group(g + 2)
            if ahead:
                for name in ("x", "exc", "inh"):
                    new_operand(n, name)
            for pop in POPS:
                turned = (g, "inh") if pop == "exc" else (n, "exc")
                for i in range(SLOTS):
                    acc = sums(g, pop, i)
                    lifted = not ahead and (pop, i) in LIFTED
                    if lifted:
                        new_state_off_vector(g, pop, i, acc)
                        relu_on_gpsimd(g, pop, i)
                    else:
                        new_state(g, pop, i, acc, whole)
                    if not ahead and not lifted:
                        relu_on_scalar(g, pop, i, whole)
                        store(g, pop, i * UNITS, (i + 1) * UNITS)
                    if not ahead and (pop, i) == ("exc", 0):
                        row_factors(g, "inh")
                        row_leak(g, "inh")
                    if not ahead and (pop, i) == ("inh", 1):
                        for late_pop, late in LIFTED:
                            store(g, late_pop, late * UNITS, (late + 1) * UNITS)
                    if g > 0 and (pop, i) == ("exc", 0):
                        quantise(g, "exc")
                    if ahead and i not in SCALAR_RELU[pop]:
                        relu_on_gpsimd(g, pop, i)
                    if ahead and (pop, i) == ("exc", 0):
                        row_product(n, "exc")
                if ahead and pop == "exc":
                    leak(*turned, 0)
                    turn(n, "x", "x", 0)
                    turn(n, "inh", "y_inh", 0)
                    leak(*turned, 1)
                    turn(n, "x", "x", 1)
                    turn(n, "inh", "y_inh", 1)
                    leak(*turned, 2)
                    turn_states(n, pop, 0)
                    leak(*turned, 3)
                    turn_states(n, pop, 1)
                    late_relus(g, pop)
                    quantise(n, "x")
                    row_factors(n, "exc")
                elif ahead:
                    row_leak(n, "exc")
                    row_product(n, "inh")
                    quantise(n, "inh")
                    leak(*turned, 0)
                    turn(n, "exc", "y_exc", 0)
                    leak(*turned, 1)
                    turn(n, "exc", "y_exc", 1)
                    leak(*turned, 2)
                    turn_states(n, pop, 0)
                    leak(*turned, 3)
                    turn_states(n, pop, 1)
                    late_relus(g, pop)
                elif pop == "exc":
                    for i in range(SLOTS):
                        leak(g, "inh", i)
